import numpy as np
import ml_dtypes


def mxq(x, axis, fmt="e4m3"):
    dtype, down = {"e4m3": (ml_dtypes.float8_e4m3fn, 7), "e5m2": (ml_dtypes.float8_e5m2, 14)}[fmt]
    v = np.moveaxis(np.asarray(x, np.float32).astype(ml_dtypes.bfloat16).astype(np.float64), axis, -1)
    blocks = v.reshape(v.shape[:-1] + (-1, 32))
    amax = np.abs(blocks).max(-1, keepdims=True)
    byte = np.maximum(np.where(amax > 0, np.frexp(amax)[1] - 1 + 127, 0) - down, 1)
    scale = np.exp2(byte - 127.0)
    codes = (blocks / scale).astype(np.float32).astype(dtype).astype(np.float64)
    return np.moveaxis((codes * scale).reshape(v.shape), -1, axis)


WIDE = False


def mx_kscale(k):
    if not WIDE:
        return np.ones(k)
    levels = np.array([10, -10, 5, -5, 0])
    a = np.random.permutation(np.resize(levels, k // 512 * 4)).reshape(k // 512, 4)
    idx = np.arange(k)
    return np.exp2(a[idx // 512, idx % 128 // 32])


BF16 = ml_dtypes.bfloat16


def bf(x):
    return np.asarray(x, np.float32).astype(BF16)


def f64(x):
    return np.asarray(x).astype(np.float64)


E2M1 = np.array([0.0, 0.5, 1.0, 1.5, 2.0, 3.0, 4.0, 6.0, -0.0, -0.5, -1.0, -1.5, -2.0, -3.0, -4.0, -6.0])


def pack_weight(w, fmt):
    k, n = w.shape
    w = f64(bf(w)).reshape(k // 32, 32, n)
    amax = np.abs(w).max(1)
    if fmt == "e4m3":
        byte = np.frexp(amax)[1] - 1 + 127 - 7
    else:
        mant, ex = np.frexp(amax / 6.0)
        byte = np.where(mant > 0.5, ex, ex - 1) + 127
    byte = np.clip(np.where(amax > 0, byte, 1), 1, 254)
    scaled = (w * np.exp2(127.0 - byte)[:, None, :]).reshape(k, n).astype(np.float32)
    by_word = np.ascontiguousarray(scaled.reshape(k // 512, 128, 4, n).transpose(0, 1, 3, 2))
    if fmt == "e4m3":
        words = by_word.astype(ml_dtypes.float8_e4m3fn).view(np.uint8)
    else:
        c = by_word.astype(ml_dtypes.float4_e2m1fn).view(np.uint8) & 0xF
        words = c[..., 0::2] | (c[..., 1::2] << 4)
    return np.ascontiguousarray(words), np.ascontiguousarray(byte.astype(np.uint8).reshape(k // 512, 16, n))


def unpack_weight(words, scales, fmt):
    g, p, n, _ = words.shape
    if fmt == "e4m3":
        vals = np.ascontiguousarray(words).view(ml_dtypes.float8_e4m3fn).astype(np.float64)
    else:
        nib = np.empty((g, p, n, 4), np.uint8)
        nib[..., 0::2] = words & 0xF
        nib[..., 1::2] = words >> 4
        vals = E2M1[nib]
    vals = vals * np.repeat(np.exp2(scales.astype(np.float64) - 127.0), 8, axis=1)[..., None]
    return vals.transpose(0, 1, 3, 2).reshape(g * 512, n)


B, N, D, F1, F2, F3, G1, G2 = 4, 32, 512, 512, 1024, 512, 512, 512
ALPHA = 0.2
FMT = "e4m3"


def lrelu(v):
    return np.maximum(v, ALPHA * v)


def setup_inputs():
    s, t = mx_kscale(F2), mx_kscale(F3 + D)
    e2 = bf(lrelu(np.random.standard_normal((B, N, N, F2))) * s)
    x = bf(np.random.standard_normal((B, N, D)) * t[F3:])
    fe_w2_words, fe_w2_scales = pack_weight(np.random.standard_normal((F2, F3)) * (12.0 / N) / np.sqrt(F2) / s[:, None] * t[:F3], FMT)
    fe_b2 = bf(np.random.standard_normal(F3) * (3.0 / N) * t[:F3])
    fn_w0_words, fn_w0_scales = pack_weight(np.random.standard_normal((F3 + D, G1)) * 0.25 / np.sqrt(F3 + D) / t[:, None], FMT)
    fn_b0 = bf(np.random.standard_normal(G1) * 0.3)
    return {"e2": e2,
            "x": x,
            "fe_w2_words": fe_w2_words,
            "fe_w2_scales": fe_w2_scales,
            "fe_b2": fe_b2,
            "fn_w0_words": fn_w0_words,
            "fn_w0_scales": fn_w0_scales,
            "fn_b0": fn_b0}


def reference(e2, x, fe_w2_words, fe_w2_scales, fe_b2, fn_w0_words, fn_w0_scales, fn_b0):
    a3 = lrelu((mxq(f64(e2), 3, "e4m3") @ unpack_weight(fe_w2_words, fe_w2_scales, FMT)) + f64(fe_b2))
    agg = a3.sum(axis=2)
    h = np.concatenate([agg, f64(x)], axis=-1)
    return lrelu((mxq(h, 2, "e4m3") @ unpack_weight(fn_w0_words, fn_w0_scales, FMT)) + f64(fn_b0))

@@ -1,0 +1,290 @@
+from contextlib import ExitStack
+
+import concourse.mybir as mybir
+from concourse.masks import make_identity
+
+F32 = mybir.dt.float32
+BF16 = mybir.dt.bfloat16
+I32 = mybir.dt.int32
+U32 = mybir.dt.uint32
+U8 = mybir.dt.uint8
+FP8X4 = mybir.dt.float8_e4m3fn_x4
+ALU = mybir.AluOpType
+ACT = mybir.ActivationFunctionType
+AXIS = mybir.AxisListType
+
+P = 128
+PACK = 4
+K_PASS = P * PACK
+PASSES = 2
+PAIRS_OF_K = 2
+WORDS = K_PASS // 2
+
+NEIGHBOURS = 32
+NODES = 128
+EDGE_K = 1024
+FEATURES = 512
+FEATURE_TILES = FEATURES // P
+
+CHUNK = 512
+ROW_TILES = CHUNK // P
+CHUNKS = NODES * NEIGHBOURS // CHUNK
+CHUNK_NODES = CHUNK // NEIGHBOURS
+HALF = CHUNK // 2
+SLOPE = 0.2
+
+FLOPS = 2 * NODES * NEIGHBOURS * EDGE_K * FEATURES + 2 * NODES * (2 * FEATURES) * FEATURES
+
+
+def tile_graph_gan_pb_kernel(
+    tc, e2, x, fe_w2_words, fe_w2_scales, fe_b2, fn_w0_words, fn_w0_scales, fn_b0, out
+):
+    nc = tc.nc
+    e2_rows = e2.rearrange("b i j k -> (b i j) k")
+    x_rows = x.rearrange("b i d -> (b i) d")
+    out_rows = out.rearrange("b i f -> (b i) f")
+
+    with ExitStack() as ctx:
+        ctx.enter_context(tc.manual_schedule())
+        keep = ctx.enter_context(tc.tile_pool(name="keep", bufs=1))
+        e2_pool = ctx.enter_context(tc.tile_pool(name="e2", bufs=CHUNKS))
+        stage = ctx.enter_context(tc.tile_pool(name="stage", bufs=2))
+        scaled_pool = ctx.enter_context(tc.tile_pool(name="scaled", bufs=FEATURE_TILES))
+        flip_banks = ctx.enter_context(tc.psum_pool(name="flip_banks", bufs=4))
+        sum_banks = ctx.enter_context(tc.psum_pool(name="sum_banks", bufs=4))
+
+        fe_words = keep.tile([P, PASSES, FEATURES], U32, align_bytes=64)
+        fe_planes = keep.tile([P, PASSES, FEATURES], U8, align_bytes=64)
+        fn_words = keep.tile([P, PASSES, FEATURES], U32, align_bytes=64)
+        fn_planes = keep.tile([P, PASSES, FEATURES], U8, align_bytes=64)
+        fe_bias_rows = keep.tile([P, P], BF16)
+        nc.vector.memset(fe_planes[:].bitcast(I32), 0)
+        nc.vector.memset(fe_bias_rows[:], 0.0)
+        nc.vector.memset(fn_planes[:].bitcast(I32), 0)
+
+        ident_f32 = keep.tile([P, P], F32)
+        make_identity(nc, ident_f32[:])
+        ident_bf16 = keep.tile([P, P], BF16)
+        make_identity(nc, ident_bf16[:])
+
+        x_sb = keep.tile([P, FEATURES], BF16)
+        nc.scalar.dma_start(out=fe_bias_rows[0:FEATURE_TILES, :], in_=fe_b2.rearrange("(m p) -> m p", p=P))
+        nc.scalar.dma_start(out=x_sb[:], in_=x_rows)
+
+        def load_weight(words_dram, scales_dram, words, planes):
+            for quadrant in range(4):
+                nc.sync.dma_start(
+                    out=planes[32 * quadrant : 32 * quadrant + 4, :, :].bitcast(I32),
+                    in_=scales_dram.bitcast(I32)[:, 4 * quadrant : 4 * quadrant + 4, :].rearrange("g r n -> r g n"),
+                )
+            nc.sync.dma_start(
+                out=words[:].bitcast(I32),
+                in_=words_dram.rearrange("g p n t -> g p (n t)").bitcast(I32).rearrange("g p n -> p g n"),
+            )
+
+        e2_tiles = []
+        for c in range(CHUNKS):
+            e2_sb = e2_pool.tile([P, ROW_TILES, EDGE_K], BF16)
+            e2_tiles.append(e2_sb)
+            rows = e2_rows[CHUNK * c : CHUNK * (c + 1), :].rearrange("(p a) k -> p a k", a=ROW_TILES)
+            if c == 0:
+                for a in range(ROW_TILES):
+                    nc.sync.dma_start(out=e2_sb[:, a, :], in_=rows[:, a, :])
+                load_weight(fe_w2_words, fe_w2_scales, fe_words, fe_planes)
+            else:
+                nc.sync.dma_start(out=e2_sb[:], in_=rows)
+        load_weight(fn_w0_words, fn_w0_scales, fn_words, fn_planes)
+        fn_bias = keep.tile([P, FEATURES], BF16)
+        nc.sync.dma_start(out=fn_bias[:], in_=fn_b0.partition_broadcast(P))
+
+        bias_flipped = flip_banks.tile([P, P], BF16, tag="flipped")
+        nc.tensor.transpose(out=bias_flipped[:], in_=fe_bias_rows[:], identity=ident_bf16[:])
+        fe_bias = keep.tile([P, FEATURE_TILES], F32)
+        nc.vector.tensor_copy(out=fe_bias[:], in_=bias_flipped[:, 0:FEATURE_TILES])
+        fe_bias_scaled = keep.tile([P, FEATURE_TILES], F32)
+        nc.vector.tensor_scalar_mul(out=fe_bias_scaled[:], in0=fe_bias[:], scalar1=SLOPE)
+
+        agg_t = keep.tile([P, FEATURE_TILES, NODES], F32)
+        h_codes = keep.tile([P, PASSES, NODES], U32, align_bytes=64)
+        h_scales = keep.tile([P, PASSES, NODES], U8, align_bytes=64)
+
+        def transpose_chunk(c):
+            words = e2_tiles[c][:].bitcast(F32)
+            banks = []
+            for a in range(ROW_TILES):
+                flipped = flip_banks.tile([P, PASSES, PAIRS_OF_K, P], F32, tag="flipped")
+                for g in range(PASSES):
+                    for u in range(PAIRS_OF_K):
+                        nc.tensor.transpose(
+                            out=flipped[:, g, u, :],
+                            in_=words[:, a, WORDS * g + u : WORDS * (g + 1) : PAIRS_OF_K],
+                            identity=ident_f32[:],
+                        )
+                banks.append(flipped)
+            return banks
+
+        def regroup_chunk(banks):
+            grouped = stage.tile([P, PASSES, CHUNK, PACK], BF16, align_bytes=64)
+            pairs = grouped[:].bitcast(F32)
+            for a in range(ROW_TILES):
+                nc.scalar.copy(
+                    out=pairs[:, :, P * a : P * (a + 1), :],
+                    in_=banks[a][:].rearrange("p g u r -> p g r u"),
+                )
+            return grouped
+
+        def quantise_chunk(grouped):
+            codes = stage.tile([P, PASSES, CHUNK], U32, align_bytes=64)
+            scales = stage.tile([P, PASSES, CHUNK], U8, align_bytes=64)
+            nc.vector.quantize_mx(
+                out=codes[:].rearrange("p g c -> p (g c)").bitcast(FP8X4),
+                scales=scales[:].rearrange("p g c -> p (g c)"),
+                in_=grouped[:].rearrange("p g c t -> p (g c t)"),
+            )
+            return codes, scales
+
+        def edge_matmuls(codes, scales):
+            banks = []
+            for m in range(FEATURE_TILES):
+                edge_sum = sum_banks.tile([P, CHUNK], F32, tag="sums")
+                for g in range(PASSES):
+                    nc.tensor.matmul_mx(
+                        out=edge_sum[:],
+                        lhsT=fe_words[:, g, P * m : P * (m + 1)].bitcast(FP8X4),
+                        lhsT_scale=fe_planes[:, g, P * m : P * (m + 1)],
+                        rhs=codes[:, g, :].bitcast(FP8X4),
+                        rhs_scale=scales[:, g, :],
+                        start=(g == 0),
+                        stop=(g == PASSES - 1),
+                    )
+                banks.append(edge_sum)
+            return banks
+
+        def scale_sums(banks):
+            scaled_tiles = []
+            for m in range(FEATURE_TILES):
+                scaled = scaled_pool.tile([P, CHUNK], F32)
+                nc.scalar.activation(
+                    out=scaled[:],
+                    in_=banks[m][:],
+                    func=ACT.Identity,
+                    bias=fe_bias_scaled[:, m : m + 1],
+                    scale=SLOPE,
+                )
+                scaled_tiles.append(scaled)
+            return scaled_tiles
+
+        def leaky_and_halve(banks, scaled_tiles):
+            a3 = stage.tile([P, FEATURE_TILES, CHUNK], F32)
+            halved = stage.tile([P, FEATURE_TILES, HALF], F32)
+            for m in range(FEATURE_TILES):
+                nc.vector.scalar_tensor_tensor(
+                    out=a3[:, m, :],
+                    in0=banks[m][:],
+                    scalar=fe_bias[:, m : m + 1],
+                    in1=scaled_tiles[m][:],
+                    op0=ALU.add,
+                    op1=ALU.max,
+                )
+            for m in range(0, FEATURE_TILES, 2):
+                nc.gpsimd.tensor_tensor(
+                    out=halved[:, m : m + 2, :],
+                    in0=a3[:, m : m + 2, 0:HALF],
+                    in1=a3[:, m : m + 2, HALF:CHUNK],
+                    op=ALU.add,
+                )
+            return halved
+
+        def sum_neighbours(c, halved):
+            nc.vector.tensor_reduce(
+                out=agg_t[:, :, CHUNK_NODES * c : CHUNK_NODES * (c + 1)],
+                in_=halved[:].rearrange("p m (a n l) -> p m n a l", a=2, n=CHUNK_NODES),
+                axis=AXIS.XY,
+                op=ALU.add,
+            )
+
+        grouped = regroup_chunk(transpose_chunk(0))
+
+        x_words = x_sb[:].bitcast(F32)
+        x_flipped = flip_banks.tile([P, PAIRS_OF_K, NODES], F32, tag="flipped")
+        for u in range(PAIRS_OF_K):
+            nc.tensor.transpose(out=x_flipped[:, u, :], in_=x_words[:, u:WORDS:PAIRS_OF_K], identity=ident_f32[:])
+        x_grouped = keep.tile([P, NODES, PACK], BF16, align_bytes=64)
+        nc.scalar.copy(out=x_grouped[:].bitcast(F32), in_=x_flipped[:].rearrange("p u r -> p r u"))
+
+        codes, scales = quantise_chunk(grouped)
+        nc.vector.quantize_mx(
+            out=h_codes[:, 1, :].bitcast(FP8X4),
+            scales=h_scales[:, 1, :],
+            in_=x_grouped[:].rearrange("p r t -> p (r t)"),
+        )
+
+        halved_before = None
+        for c in range(CHUNKS):
+            more = c + 1 < CHUNKS
+            if more:
+                flipped_banks = transpose_chunk(c + 1)
+            edge_banks = edge_matmuls(codes, scales)
+            if more:
+                grouped = regroup_chunk(flipped_banks)
+            scaled_tiles = scale_sums(edge_banks)
+            if more:
+                codes, scales = quantise_chunk(grouped)
+            if c > 0:
+                sum_neighbours(c - 1, halved_before)
+            halved_before = leaky_and_halve(edge_banks, scaled_tiles)
+        sum_neighbours(CHUNKS - 1, halved_before)
+
+        node_sum = sum_banks.tile([P, FEATURES], F32, tag="sums")
+
+        def node_matmul(g, first, last):
+            nc.tensor.matmul_mx(
+                out=node_sum[:],
+                lhsT=h_codes[:, g, :].bitcast(FP8X4),
+                lhsT_scale=h_scales[:, g, :],
+                rhs=fn_words[:, g, :].bitcast(FP8X4),
+                rhs_scale=fn_planes[:, g, :],
+                start=first,
+                stop=last,
+            )
+
+        node_matmul(1, True, False)
+
+        agg_bf16 = keep.tile([P, FEATURES], BF16)
+        for half in range(2):
+            agg_rows = flip_banks.tile([P, 2, P], F32, tag="flipped")
+            for m in range(2):
+                nc.tensor.transpose(out=agg_rows[:, m, :], in_=agg_t[:, 2 * half + m, :], identity=ident_f32[:])
+            rounded = agg_bf16[:, HALF * half : HALF * (half + 1)]
+            if half == 0:
+                nc.scalar.copy(out=rounded, in_=agg_rows[:].rearrange("p m f -> p (m f)"))
+            else:
+                nc.vector.tensor_copy(out=rounded, in_=agg_rows[:].rearrange("p m f -> p (m f)"))
+        agg_flipped = flip_banks.tile([P, PACK, NODES], BF16, tag="flipped")
+        for t in range(PACK):
+            nc.tensor.transpose(out=agg_flipped[:, t, :], in_=agg_bf16[:, t:FEATURES:PACK], identity=ident_bf16[:])
+        agg_grouped = keep.tile([P, NODES, PACK], BF16, align_bytes=64)
+        nc.vector.tensor_copy(out=agg_grouped[:], in_=agg_flipped[:].rearrange("p t r -> p r t"))
+        nc.vector.quantize_mx(
+            out=h_codes[:, 0, :].bitcast(FP8X4),
+            scales=h_scales[:, 0, :],
+            in_=agg_grouped[:].rearrange("p r t -> p (r t)"),
+        )
+        node_matmul(0, False, True)
+
+        biased = keep.tile([P, FEATURES], F32)
+        result = keep.tile([P, FEATURES], F32)
+        for half in range(2):
+            cols = slice(HALF * half, HALF * (half + 1))
+            nc.vector.tensor_tensor(out=biased[:, cols], in0=node_sum[:, cols], in1=fn_bias[:, cols], op=ALU.add)
+        for half in range(2):
+            cols = slice(HALF * half, HALF * (half + 1))
+            nc.vector.scalar_tensor_tensor(
+                out=result[:, cols],
+                in0=biased[:, cols],
+                scalar=SLOPE,
+                in1=biased[:, cols],
+                op0=ALU.mult,
+                op1=ALU.max,
+            )
+            nc.sync.dma_start(out=out_rows[:, cols], in_=result[:, cols])

@@ -108,10 +108,10 @@ def tile_graph_gan_pb_kernel(
         h_codes = keep.tile([P, PASSES, NODES], U32, align_bytes=64)
         h_scales = keep.tile([P, PASSES, NODES], U8, align_bytes=64)
 
-        def transpose_chunk(c):
+        def transpose_rows(c, h):
             words = e2_tiles[c][:].bitcast(F32)
             banks = []
-            for a in range(ROW_TILES):
+            for a in range(2 * h, 2 * h + 2):
                 flipped = flip_banks.tile([P, PASSES, PAIRS_OF_K, P], F32, tag="flipped")
                 for g in range(PASSES):
                     for u in range(PAIRS_OF_K):
@@ -123,15 +123,14 @@ def tile_graph_gan_pb_kernel(
                 banks.append(flipped)
             return banks
 
-        def regroup_chunk(banks):
-            grouped = stage.tile([P, PASSES, CHUNK, PACK], BF16, align_bytes=64)
+        def regroup_rows(grouped, h, banks):
             pairs = grouped[:].bitcast(F32)
-            for a in range(ROW_TILES):
+            for i in range(2):
+                a = 2 * h + i
                 nc.scalar.copy(
                     out=pairs[:, :, P * a : P * (a + 1), :],
-                    in_=banks[a][:].rearrange("p g u r -> p g r u"),
+                    in_=banks[i][:].rearrange("p g u r -> p g r u"),
                 )
-            return grouped
 
         def quantise_chunk(grouped):
             codes = stage.tile([P, PASSES, CHUNK], U32, align_bytes=64)
@@ -143,9 +142,9 @@ def tile_graph_gan_pb_kernel(
             )
             return codes, scales
 
-        def edge_matmuls(codes, scales):
+        def edge_matmuls(codes, scales, h):
             banks = []
-            for m in range(FEATURE_TILES):
+            for m in range(2 * h, 2 * h + 2):
                 edge_sum = sum_banks.tile([P, CHUNK], F32, tag="sums")
                 for g in range(PASSES):
                     nc.tensor.matmul_mx(
@@ -160,13 +159,14 @@ def tile_graph_gan_pb_kernel(
                 banks.append(edge_sum)
             return banks
 
-        def scale_sums(banks):
+        def scale_sums(banks, h):
             scaled_tiles = []
-            for m in range(FEATURE_TILES):
+            for i in range(2):
+                m = 2 * h + i
                 scaled = scaled_pool.tile([P, CHUNK], F32)
                 nc.scalar.activation(
                     out=scaled[:],
-                    in_=banks[m][:],
+                    in_=banks[i][:],
                     func=ACT.Identity,
                     bias=fe_bias_scaled[:, m : m + 1],
                     scale=SLOPE,
@@ -174,36 +174,33 @@ def tile_graph_gan_pb_kernel(
                 scaled_tiles.append(scaled)
             return scaled_tiles
 
-        def leaky_and_halve(banks, scaled_tiles):
-            a3 = stage.tile([P, FEATURE_TILES, CHUNK], F32)
-            halved = stage.tile([P, FEATURE_TILES, HALF], F32)
-            for m in range(FEATURE_TILES):
+        def leaky_and_halve(banks, scaled_tiles, h):
+            a3 = stage.tile([P, 2, CHUNK], F32)
+            halved = stage.tile([P, 2, HALF], F32)
+            for i in range(2):
+                m = 2 * h + i
                 nc.vector.scalar_tensor_tensor(
-                    out=a3[:, m, :],
-                    in0=banks[m][:],
+                    out=a3[:, i, :],
+                    in0=banks[i][:],
                     scalar=fe_bias[:, m : m + 1],
-                    in1=scaled_tiles[m][:],
+                    in1=scaled_tiles[i][:],
                     op0=ALU.add,
                     op1=ALU.max,
                 )
-            for m in range(0, FEATURE_TILES, 2):
-                nc.gpsimd.tensor_tensor(
-                    out=halved[:, m : m + 2, :],
-                    in0=a3[:, m : m + 2, 0:HALF],
-                    in1=a3[:, m : m + 2, HALF:CHUNK],
-                    op=ALU.add,
-                )
+            nc.gpsimd.tensor_tensor(out=halved[:], in0=a3[:, :, 0:HALF], in1=a3[:, :, HALF:CHUNK], op=ALU.add)
             return halved
 
-        def sum_neighbours(c, halved):
+        def sum_neighbours(c, h, halved):
             nc.vector.tensor_reduce(
-                out=agg_t[:, :, CHUNK_NODES * c : CHUNK_NODES * (c + 1)],
+                out=agg_t[:, 2 * h : 2 * h + 2, CHUNK_NODES * c : CHUNK_NODES * (c + 1)],
                 in_=halved[:].rearrange("p m (a n l) -> p m n a l", a=2, n=CHUNK_NODES),
                 axis=AXIS.XY,
                 op=ALU.add,
             )
 
-        grouped = regroup_chunk(transpose_chunk(0))
+        grouped = stage.tile([P, PASSES, CHUNK, PACK], BF16, align_bytes=64)
+        for h in range(2):
+            regroup_rows(grouped, h, transpose_rows(0, h))
 
         x_words = x_sb[:].bitcast(F32)
         x_flipped = flip_banks.tile([P, PAIRS_OF_K, NODES], F32, tag="flipped")
@@ -219,21 +216,28 @@ def tile_graph_gan_pb_kernel(
             in_=x_grouped[:].rearrange("p r t -> p (r t)"),
         )
 
-        halved_before = None
+        waiting = None
         for c in range(CHUNKS):
             more = c + 1 < CHUNKS
+            next_codes = None
             if more:
-                flipped_banks = transpose_chunk(c + 1)
-            edge_banks = edge_matmuls(codes, scales)
+                grouped = stage.tile([P, PASSES, CHUNK, PACK], BF16, align_bytes=64)
+            for h in range(2):
+                if more:
+                    flipped_banks = transpose_rows(c + 1, h)
+                edge_banks = edge_matmuls(codes, scales, h)
+                if more:
+                    regroup_rows(grouped, h, flipped_banks)
+                scaled_tiles = scale_sums(edge_banks, h)
+                if more and h == 1:
+                    next_codes = quantise_chunk(grouped)
+                halved = leaky_and_halve(edge_banks, scaled_tiles, h)
+                if waiting is not None:
+                    sum_neighbours(*waiting)
+                waiting = (c, h, halved)
             if more:
-                grouped = regroup_chunk(flipped_banks)
-            scaled_tiles = scale_sums(edge_banks)
-            if more:
-                codes, scales = quantise_chunk(grouped)
-            if c > 0:
-                sum_neighbours(c - 1, halved_before)
-            halved_before = leaky_and_halve(edge_banks, scaled_tiles)
-        sum_neighbours(CHUNKS - 1, halved_before)
+                codes, scales = next_codes
+        sum_neighbours(*waiting)
 
         node_sum = sum_banks.tile([P, FEATURES], F32, tag="sums")
 

@@ -174,9 +174,8 @@ def tile_graph_gan_pb_kernel(
                 scaled_tiles.append(scaled)
             return scaled_tiles
 
-        def leaky_and_halve(banks, scaled_tiles, h):
+        def leaky_relu(banks, scaled_tiles, h):
             a3 = stage.tile([P, 2, CHUNK], F32)
-            halved = stage.tile([P, 2, HALF], F32)
             for i in range(2):
                 m = 2 * h + i
                 nc.vector.scalar_tensor_tensor(
@@ -187,13 +186,12 @@ def tile_graph_gan_pb_kernel(
                     op0=ALU.add,
                     op1=ALU.max,
                 )
-            nc.gpsimd.tensor_tensor(out=halved[:], in0=a3[:, :, 0:HALF], in1=a3[:, :, HALF:CHUNK], op=ALU.add)
-            return halved
+            return a3
 
-        def sum_neighbours(c, h, halved):
+        def sum_neighbours(c, h, a3):
             nc.vector.tensor_reduce(
                 out=agg_t[:, 2 * h : 2 * h + 2, CHUNK_NODES * c : CHUNK_NODES * (c + 1)],
-                in_=halved[:].rearrange("p m (a n l) -> p m n a l", a=2, n=CHUNK_NODES),
+                in_=a3[:].rearrange("p m (a n l) -> p m n a l", a=ROW_TILES, n=CHUNK_NODES),
                 axis=AXIS.XY,
                 op=ALU.add,
             )
@@ -231,10 +229,10 @@ def tile_graph_gan_pb_kernel(
                 scaled_tiles = scale_sums(edge_banks, h)
                 if more and h == 1:
                     next_codes = quantise_chunk(grouped)
-                halved = leaky_and_halve(edge_banks, scaled_tiles, h)
+                a3 = leaky_relu(edge_banks, scaled_tiles, h)
                 if waiting is not None:
                     sum_neighbours(*waiting)
-                waiting = (c, h, halved)
+                waiting = (c, h, a3)
             if more:
                 codes, scales = next_codes
         sum_neighbours(*waiting)

@@ -108,29 +108,23 @@ def tile_graph_gan_pb_kernel(
         h_codes = keep.tile([P, PASSES, NODES], U32, align_bytes=64)
         h_scales = keep.tile([P, PASSES, NODES], U8, align_bytes=64)
 
-        def transpose_rows(c, h):
+        def transpose_rows(c, a):
             words = e2_tiles[c][:].bitcast(F32)
-            banks = []
-            for a in range(2 * h, 2 * h + 2):
-                flipped = flip_banks.tile([P, PASSES, PAIRS_OF_K, P], F32, tag="flipped")
-                for g in range(PASSES):
-                    for u in range(PAIRS_OF_K):
-                        nc.tensor.transpose(
-                            out=flipped[:, g, u, :],
-                            in_=words[:, a, WORDS * g + u : WORDS * (g + 1) : PAIRS_OF_K],
-                            identity=ident_f32[:],
-                        )
-                banks.append(flipped)
-            return banks
+            flipped = flip_banks.tile([P, PASSES, PAIRS_OF_K, P], F32, tag="flipped")
+            for g in range(PASSES):
+                for u in range(PAIRS_OF_K):
+                    nc.tensor.transpose(
+                        out=flipped[:, g, u, :],
+                        in_=words[:, a, WORDS * g + u : WORDS * (g + 1) : PAIRS_OF_K],
+                        identity=ident_f32[:],
+                    )
+            return flipped
 
-        def regroup_rows(grouped, h, banks):
-            pairs = grouped[:].bitcast(F32)
-            for i in range(2):
-                a = 2 * h + i
-                nc.scalar.copy(
-                    out=pairs[:, :, P * a : P * (a + 1), :],
-                    in_=banks[i][:].rearrange("p g u r -> p g r u"),
-                )
+        def regroup_rows(grouped, a, flipped):
+            nc.scalar.copy(
+                out=grouped[:].bitcast(F32)[:, :, P * a : P * (a + 1), :],
+                in_=flipped[:].rearrange("p g u r -> p g r u"),
+            )
 
         def quantise_chunk(grouped):
             codes = stage.tile([P, PASSES, CHUNK], U32, align_bytes=64)
@@ -142,63 +136,54 @@ def tile_graph_gan_pb_kernel(
             )
             return codes, scales
 
-        def edge_matmuls(codes, scales, h):
-            banks = []
-            for m in range(2 * h, 2 * h + 2):
-                edge_sum = sum_banks.tile([P, CHUNK], F32, tag="sums")
-                for g in range(PASSES):
-                    nc.tensor.matmul_mx(
-                        out=edge_sum[:],
-                        lhsT=fe_words[:, g, P * m : P * (m + 1)].bitcast(FP8X4),
-                        lhsT_scale=fe_planes[:, g, P * m : P * (m + 1)],
-                        rhs=codes[:, g, :].bitcast(FP8X4),
-                        rhs_scale=scales[:, g, :],
-                        start=(g == 0),
-                        stop=(g == PASSES - 1),
-                    )
-                banks.append(edge_sum)
-            return banks
-
-        def scale_sums(banks, h):
-            scaled_tiles = []
-            for i in range(2):
-                m = 2 * h + i
-                scaled = scaled_pool.tile([P, CHUNK], F32)
-                nc.scalar.activation(
-                    out=scaled[:],
-                    in_=banks[i][:],
-                    func=ACT.Identity,
-                    bias=fe_bias_scaled[:, m : m + 1],
-                    scale=SLOPE,
+        def edge_matmul(codes, scales, m):
+            edge_sum = sum_banks.tile([P, CHUNK], F32, tag="sums")
+            for g in range(PASSES):
+                nc.tensor.matmul_mx(
+                    out=edge_sum[:],
+                    lhsT=fe_words[:, g, P * m : P * (m + 1)].bitcast(FP8X4),
+                    lhsT_scale=fe_planes[:, g, P * m : P * (m + 1)],
+                    rhs=codes[:, g, :].bitcast(FP8X4),
+                    rhs_scale=scales[:, g, :],
+                    start=(g == 0),
+                    stop=(g == PASSES - 1),
                 )
-                scaled_tiles.append(scaled)
-            return scaled_tiles
+            return edge_sum
 
-        def leaky_relu(banks, scaled_tiles, h):
-            a3 = stage.tile([P, 2, CHUNK], F32)
-            for i in range(2):
-                m = 2 * h + i
-                nc.vector.scalar_tensor_tensor(
-                    out=a3[:, i, :],
-                    in0=banks[i][:],
-                    scalar=fe_bias[:, m : m + 1],
-                    in1=scaled_tiles[i][:],
-                    op0=ALU.add,
-                    op1=ALU.max,
-                )
+        def scale_sum(edge_sum, m):
+            scaled = scaled_pool.tile([P, CHUNK], F32)
+            nc.scalar.activation(
+                out=scaled[:],
+                in_=edge_sum[:],
+                func=ACT.Identity,
+                bias=fe_bias_scaled[:, m : m + 1],
+                scale=SLOPE,
+            )
+            return scaled
+
+        def leaky_relu(edge_sum, scaled, m):
+            a3 = stage.tile([P, CHUNK], F32)
+            nc.vector.scalar_tensor_tensor(
+                out=a3[:],
+                in0=edge_sum[:],
+                scalar=fe_bias[:, m : m + 1],
+                in1=scaled[:],
+                op0=ALU.add,
+                op1=ALU.max,
+            )
             return a3
 
-        def sum_neighbours(c, h, a3):
+        def sum_neighbours(c, m, a3):
             nc.vector.tensor_reduce(
-                out=agg_t[:, 2 * h : 2 * h + 2, CHUNK_NODES * c : CHUNK_NODES * (c + 1)],
-                in_=a3[:].rearrange("p m (a n l) -> p m n a l", a=ROW_TILES, n=CHUNK_NODES),
+                out=agg_t[:, m, CHUNK_NODES * c : CHUNK_NODES * (c + 1)],
+                in_=a3[:].rearrange("p (a n l) -> p n a l", a=ROW_TILES, n=CHUNK_NODES),
                 axis=AXIS.XY,
                 op=ALU.add,
             )
 
         grouped = stage.tile([P, PASSES, CHUNK, PACK], BF16, align_bytes=64)
-        for h in range(2):
-            regroup_rows(grouped, h, transpose_rows(0, h))
+        for a in range(ROW_TILES):
+            regroup_rows(grouped, a, transpose_rows(0, a))
 
         x_words = x_sb[:].bitcast(F32)
         x_flipped = flip_banks.tile([P, PAIRS_OF_K, NODES], F32, tag="flipped")
@@ -214,25 +199,26 @@ def tile_graph_gan_pb_kernel(
             in_=x_grouped[:].rearrange("p r t -> p (r t)"),
         )
 
+        assert ROW_TILES == FEATURE_TILES
         waiting = None
         for c in range(CHUNKS):
             more = c + 1 < CHUNKS
             next_codes = None
             if more:
                 grouped = stage.tile([P, PASSES, CHUNK, PACK], BF16, align_bytes=64)
-            for h in range(2):
+            for q in range(FEATURE_TILES):
                 if more:
-                    flipped_banks = transpose_rows(c + 1, h)
-                edge_banks = edge_matmuls(codes, scales, h)
+                    flipped = transpose_rows(c + 1, q)
+                edge_sum = edge_matmul(codes, scales, q)
                 if more:
-                    regroup_rows(grouped, h, flipped_banks)
-                scaled_tiles = scale_sums(edge_banks, h)
-                if more and h == 1:
+                    regroup_rows(grouped, q, flipped)
+                scaled = scale_sum(edge_sum, q)
+                if more and q == ROW_TILES - 1:
                     next_codes = quantise_chunk(grouped)
-                a3 = leaky_relu(edge_banks, scaled_tiles, h)
+                a3 = leaky_relu(edge_sum, scaled, q)
                 if waiting is not None:
                     sum_neighbours(*waiting)
-                waiting = (c, h, a3)
+                waiting = (c, q, a3)
             if more:
                 codes, scales = next_codes
         sum_neighbours(*waiting)

@@ -26,11 +26,11 @@ EDGE_K = 1024
 FEATURES = 512
 FEATURE_TILES = FEATURES // P
 
-CHUNK = 512
-ROW_TILES = CHUNK // P
-CHUNKS = NODES * NEIGHBOURS // CHUNK
-CHUNK_NODES = CHUNK // NEIGHBOURS
-HALF = CHUNK // 2
+CHUNK_TILES = [2, 2] + [4] * 6 + [2, 2]
+CHUNKS = len(CHUNK_TILES)
+TILE_NODES = P // NEIGHBOURS
+assert P * sum(CHUNK_TILES) == NODES * NEIGHBOURS
+HALF = FEATURES // 2
 SLOPE = 0.2
 
 FLOPS = 2 * NODES * NEIGHBOURS * EDGE_K * FEATURES + 2 * NODES * (2 * FEATURES) * FEATURES
@@ -84,18 +84,113 @@ def tile_graph_gan_pb_kernel(
 
         e2_tiles = []
         for c in range(CHUNKS):
-            e2_sb = e2_pool.tile([P, ROW_TILES, EDGE_K], BF16)
+            tiles = CHUNK_TILES[c]
+            first_row = P * sum(CHUNK_TILES[:c])
+            e2_sb = e2_pool.tile([P, tiles, EDGE_K], BF16, tag="e2")
             e2_tiles.append(e2_sb)
-            rows = e2_rows[CHUNK * c : CHUNK * (c + 1), :].rearrange("(p a) k -> p a k", a=ROW_TILES)
+            rows = e2_rows[first_row : first_row + P * tiles, :].rearrange("(p a) k -> p a k", a=tiles)
+            for a in range(tiles):
+                nc.sync.dma_start(out=e2_sb[:, a, :], in_=rows[:, a, :])
             if c == 0:
-                for a in range(ROW_TILES):
-                    nc.sync.dma_start(out=e2_sb[:, a, :], in_=rows[:, a, :])
                 load_weight(fe_w2_words, fe_w2_scales, fe_words, fe_planes)
-            else:
-                nc.sync.dma_start(out=e2_sb[:], in_=rows)
         load_weight(fn_w0_words, fn_w0_scales, fn_words, fn_planes)
         fn_bias = keep.tile([P, FEATURES], BF16)
         nc.sync.dma_start(out=fn_bias[:], in_=fn_b0.partition_broadcast(P))
+
+        agg_t = keep.tile([P, FEATURE_TILES, NODES], F32)
+        h_codes = keep.tile([P, PASSES, NODES], U32, align_bytes=64)
+        h_scales = keep.tile([P, PASSES, NODES], U8, align_bytes=64)
+
+        def transpose_chunk(c):
+            words = e2_tiles[c][:].bitcast(F32)
+            banks = []
+            for a in range(CHUNK_TILES[c]):
+                flipped = flip_banks.tile([P, PASSES, PAIRS_OF_K, P], F32, tag="flipped")
+                for g in range(PASSES):
+                    for u in range(PAIRS_OF_K):
+                        nc.tensor.transpose(
+                            out=flipped[:, g, u, :],
+                            in_=words[:, a, WORDS * g + u : WORDS * (g + 1) : PAIRS_OF_K],
+                            identity=ident_f32[:],
+                        )
+                banks.append(flipped)
+            return banks
+
+        def regroup_chunk(c, banks):
+            grouped = stage.tile([P, PASSES, P * CHUNK_TILES[c], PACK], BF16, tag="grouped", align_bytes=64)
+            for a in range(CHUNK_TILES[c]):
+                nc.scalar.copy(
+                    out=grouped[:].bitcast(F32)[:, :, P * a : P * (a + 1), :],
+                    in_=banks[a][:].rearrange("p g u r -> p g r u"),
+                )
+            return grouped
+
+        def quantise_chunk(c, grouped):
+            codes = stage.tile([P, PASSES, P * CHUNK_TILES[c]], U32, tag="codes", align_bytes=64)
+            scales = stage.tile([P, PASSES, P * CHUNK_TILES[c]], U8, tag="scales", align_bytes=64)
+            nc.vector.quantize_mx(
+                out=codes[:].rearrange("p g c -> p (g c)").bitcast(FP8X4),
+                scales=scales[:].rearrange("p g c -> p (g c)"),
+                in_=grouped[:].rearrange("p g c t -> p (g c t)"),
+            )
+            return codes, scales
+
+        def edge_matmuls(c, codes, scales):
+            banks = []
+            for m in range(FEATURE_TILES):
+                edge_sum = sum_banks.tile([P, P * CHUNK_TILES[c]], F32, tag="sums")
+                for g in range(PASSES):
+                    nc.tensor.matmul_mx(
+                        out=edge_sum[:],
+                        lhsT=fe_words[:, g, P * m : P * (m + 1)].bitcast(FP8X4),
+                        lhsT_scale=fe_planes[:, g, P * m : P * (m + 1)],
+                        rhs=codes[:, g, :].bitcast(FP8X4),
+                        rhs_scale=scales[:, g, :],
+                        start=(g == 0),
+                        stop=(g == PASSES - 1),
+                    )
+                banks.append(edge_sum)
+            return banks
+
+        def scale_sums(c, edge_sums):
+            scaled_tiles = []
+            for m in range(FEATURE_TILES):
+                scaled = scaled_pool.tile([P, P * CHUNK_TILES[c]], F32, tag="scaled")
+                nc.scalar.activation(
+                    out=scaled[:],
+                    in_=edge_sums[m][:],
+                    func=ACT.Identity,
+                    bias=fe_bias_scaled[:, m : m + 1],
+                    scale=SLOPE,
+                )
+                scaled_tiles.append(scaled)
+            return scaled_tiles
+
+        def leaky_relu(c, edge_sums, scaled_tiles, pair):
+            a3 = stage.tile([P, 2, P * CHUNK_TILES[c]], F32, tag="a3")
+            for i in range(2):
+                m = 2 * pair + i
+                nc.vector.scalar_tensor_tensor(
+                    out=a3[:, i, :],
+                    in0=edge_sums[m][:],
+                    scalar=fe_bias[:, m : m + 1],
+                    in1=scaled_tiles[m][:],
+                    op0=ALU.add,
+                    op1=ALU.max,
+                )
+            return a3
+
+        def sum_neighbours(c, pair, a3):
+            first_node = TILE_NODES * sum(CHUNK_TILES[:c])
+            nodes = TILE_NODES * CHUNK_TILES[c]
+            nc.vector.tensor_reduce(
+                out=agg_t[:, 2 * pair : 2 * pair + 2, first_node : first_node + nodes],
+                in_=a3[:].rearrange("p m (a n l) -> p m n a l", a=CHUNK_TILES[c], n=nodes),
+                axis=AXIS.XY,
+                op=ALU.add,
+            )
+
+        grouped = regroup_chunk(0, transpose_chunk(0))
 
         bias_flipped = flip_banks.tile([P, P], BF16, tag="flipped")
         nc.tensor.transpose(out=bias_flipped[:], in_=fe_bias_rows[:], identity=ident_bf16[:])
@@ -104,87 +199,6 @@ def tile_graph_gan_pb_kernel(
         fe_bias_scaled = keep.tile([P, FEATURE_TILES], F32)
         nc.vector.tensor_scalar_mul(out=fe_bias_scaled[:], in0=fe_bias[:], scalar1=SLOPE)
 
-        agg_t = keep.tile([P, FEATURE_TILES, NODES], F32)
-        h_codes = keep.tile([P, PASSES, NODES], U32, align_bytes=64)
-        h_scales = keep.tile([P, PASSES, NODES], U8, align_bytes=64)
-
-        def transpose_rows(c, a):
-            words = e2_tiles[c][:].bitcast(F32)
-            flipped = flip_banks.tile([P, PASSES, PAIRS_OF_K, P], F32, tag="flipped")
-            for g in range(PASSES):
-                for u in range(PAIRS_OF_K):
-                    nc.tensor.transpose(
-                        out=flipped[:, g, u, :],
-                        in_=words[:, a, WORDS * g + u : WORDS * (g + 1) : PAIRS_OF_K],
-                        identity=ident_f32[:],
-                    )
-            return flipped
-
-        def regroup_rows(grouped, a, flipped):
-            nc.scalar.copy(
-                out=grouped[:].bitcast(F32)[:, :, P * a : P * (a + 1), :],
-                in_=flipped[:].rearrange("p g u r -> p g r u"),
-            )
-
-        def quantise_chunk(grouped):
-            codes = stage.tile([P, PASSES, CHUNK], U32, align_bytes=64)
-            scales = stage.tile([P, PASSES, CHUNK], U8, align_bytes=64)
-            nc.vector.quantize_mx(
-                out=codes[:].rearrange("p g c -> p (g c)").bitcast(FP8X4),
-                scales=scales[:].rearrange("p g c -> p (g c)"),
-                in_=grouped[:].rearrange("p g c t -> p (g c t)"),
-            )
-            return codes, scales
-
-        def edge_matmul(codes, scales, m):
-            edge_sum = sum_banks.tile([P, CHUNK], F32, tag="sums")
-            for g in range(PASSES):
-                nc.tensor.matmul_mx(
-                    out=edge_sum[:],
-                    lhsT=fe_words[:, g, P * m : P * (m + 1)].bitcast(FP8X4),
-                    lhsT_scale=fe_planes[:, g, P * m : P * (m + 1)],
-                    rhs=codes[:, g, :].bitcast(FP8X4),
-                    rhs_scale=scales[:, g, :],
-                    start=(g == 0),
-                    stop=(g == PASSES - 1),
-                )
-            return edge_sum
-
-        def scale_sum(edge_sum, m):
-            scaled = scaled_pool.tile([P, CHUNK], F32)
-            nc.scalar.activation(
-                out=scaled[:],
-                in_=edge_sum[:],
-                func=ACT.Identity,
-                bias=fe_bias_scaled[:, m : m + 1],
-                scale=SLOPE,
-            )
-            return scaled
-
-        def leaky_relu(edge_sum, scaled, m):
-            a3 = stage.tile([P, CHUNK], F32)
-            nc.vector.scalar_tensor_tensor(
-                out=a3[:],
-                in0=edge_sum[:],
-                scalar=fe_bias[:, m : m + 1],
-                in1=scaled[:],
-                op0=ALU.add,
-                op1=ALU.max,
-            )
-            return a3
-
-        def sum_neighbours(c, m, a3):
-            nc.vector.tensor_reduce(
-                out=agg_t[:, m, CHUNK_NODES * c : CHUNK_NODES * (c + 1)],
-                in_=a3[:].rearrange("p (a n l) -> p n a l", a=ROW_TILES, n=CHUNK_NODES),
-                axis=AXIS.XY,
-                op=ALU.add,
-            )
-
-        grouped = stage.tile([P, PASSES, CHUNK, PACK], BF16, align_bytes=64)
-        for a in range(ROW_TILES):
-            regroup_rows(grouped, a, transpose_rows(0, a))
-
         x_words = x_sb[:].bitcast(F32)
         x_flipped = flip_banks.tile([P, PAIRS_OF_K, NODES], F32, tag="flipped")
         for u in range(PAIRS_OF_K):
@@ -192,35 +206,29 @@ def tile_graph_gan_pb_kernel(
         x_grouped = keep.tile([P, NODES, PACK], BF16, align_bytes=64)
         nc.scalar.copy(out=x_grouped[:].bitcast(F32), in_=x_flipped[:].rearrange("p u r -> p r u"))
 
-        codes, scales = quantise_chunk(grouped)
+        codes, scales = quantise_chunk(0, grouped)
         nc.vector.quantize_mx(
             out=h_codes[:, 1, :].bitcast(FP8X4),
             scales=h_scales[:, 1, :],
             in_=x_grouped[:].rearrange("p r t -> p (r t)"),
         )
 
-        assert ROW_TILES == FEATURE_TILES
         waiting = None
         for c in range(CHUNKS):
             more = c + 1 < CHUNKS
-            next_codes = None
             if more:
-                grouped = stage.tile([P, PASSES, CHUNK, PACK], BF16, align_bytes=64)
-            for q in range(FEATURE_TILES):
-                if more:
-                    flipped = transpose_rows(c + 1, q)
-                edge_sum = edge_matmul(codes, scales, q)
-                if more:
-                    regroup_rows(grouped, q, flipped)
-                scaled = scale_sum(edge_sum, q)
-                if more and q == ROW_TILES - 1:
-                    next_codes = quantise_chunk(grouped)
-                a3 = leaky_relu(edge_sum, scaled, q)
+                flipped_banks = transpose_chunk(c + 1)
+            edge_sums = edge_matmuls(c, codes, scales)
+            if more:
+                grouped = regroup_chunk(c + 1, flipped_banks)
+            scaled_tiles = scale_sums(c, edge_sums)
+            if more:
+                codes, scales = quantise_chunk(c + 1, grouped)
+            for pair in range(FEATURE_TILES // 2):
+                a3 = leaky_relu(c, edge_sums, scaled_tiles, pair)
                 if waiting is not None:
                     sum_neighbours(*waiting)
-                waiting = (c, q, a3)
-            if more:
-                codes, scales = next_codes
+                waiting = (c, pair, a3)
         sum_neighbours(*waiting)
 
         node_sum = sum_banks.tile([P, FEATURES], F32, tag="sums")

@@ -28,6 +28,7 @@ FEATURE_TILES = FEATURES // P
 
 CHUNK_TILES = [2, 2] + [4] * 6 + [2, 2]
 CHUNKS = len(CHUNK_TILES)
+FOLDED_TILES = 4
 TILE_NODES = P // NEIGHBOURS
 assert P * sum(CHUNK_TILES) == NODES * NEIGHBOURS
 HALF = FEATURES // 2
@@ -178,14 +179,19 @@ def tile_graph_gan_pb_kernel(
                     op0=ALU.add,
                     op1=ALU.max,
                 )
+            if CHUNK_TILES[c] == FOLDED_TILES:
+                kept = slice(P * (FOLDED_TILES - 2), P * (FOLDED_TILES - 1))
+                folded = slice(P * (FOLDED_TILES - 1), P * FOLDED_TILES)
+                nc.gpsimd.tensor_tensor(out=a3[:, :, kept], in0=a3[:, :, kept], in1=a3[:, :, folded], op=ALU.add)
             return a3
 
         def sum_neighbours(c, pair, a3):
             first_node = TILE_NODES * sum(CHUNK_TILES[:c])
             nodes = TILE_NODES * CHUNK_TILES[c]
+            left = CHUNK_TILES[c] - 1 if CHUNK_TILES[c] == FOLDED_TILES else CHUNK_TILES[c]
             nc.vector.tensor_reduce(
                 out=agg_t[:, 2 * pair : 2 * pair + 2, first_node : first_node + nodes],
-                in_=a3[:].rearrange("p m (a n l) -> p m n a l", a=CHUNK_TILES[c], n=nodes),
+                in_=a3[:, :, 0 : P * left].rearrange("p m (a n l) -> p m n a l", a=left, n=nodes),
                 axis=AXIS.XY,
                 op=ALU.add,
             )

@@ -11,7 +11,6 @@ U8 = mybir.dt.uint8
 FP8X4 = mybir.dt.float8_e4m3fn_x4
 ALU = mybir.AluOpType
 ACT = mybir.ActivationFunctionType
-AXIS = mybir.AxisListType
 
 P = 128
 PACK = 4
@@ -28,9 +27,10 @@ FEATURE_TILES = FEATURES // P
 
 CHUNK_TILES = [2, 2] + [4] * 6 + [2, 2]
 CHUNKS = len(CHUNK_TILES)
-FOLDED_TILES = 4
-TILE_NODES = P // NEIGHBOURS
-assert P * sum(CHUNK_TILES) == NODES * NEIGHBOURS
+SLOTS = 4
+assert sum(CHUNK_TILES) == NEIGHBOURS
+VECTOR_ONLY_CHUNKS = 1
+SHARED_TILES = [1, 2, 3]
 HALF = FEATURES // 2
 SLOPE = 0.2
 
@@ -41,35 +41,41 @@ def tile_graph_gan_pb_kernel(
     tc, e2, x, fe_w2_words, fe_w2_scales, fe_b2, fn_w0_words, fn_w0_scales, fn_b0, out
 ):
     nc = tc.nc
-    e2_rows = e2.rearrange("b i j k -> (b i j) k")
+    e2_nodes = e2.rearrange("b i j k -> (b i) j k")
     x_rows = x.rearrange("b i d -> (b i) d")
     out_rows = out.rearrange("b i f -> (b i) f")
+
+    def shared(c):
+        return SHARED_TILES if c < CHUNKS - VECTOR_ONLY_CHUNKS else []
 
     with ExitStack() as ctx:
         ctx.enter_context(tc.manual_schedule())
         keep = ctx.enter_context(tc.tile_pool(name="keep", bufs=1))
         e2_pool = ctx.enter_context(tc.tile_pool(name="e2", bufs=CHUNKS))
         stage = ctx.enter_context(tc.tile_pool(name="stage", bufs=2))
-        scaled_pool = ctx.enter_context(tc.tile_pool(name="scaled", bufs=FEATURE_TILES))
+        relu_pool = ctx.enter_context(tc.tile_pool(name="relu", bufs=2 * len(SHARED_TILES)))
         flip_banks = ctx.enter_context(tc.psum_pool(name="flip_banks", bufs=4))
         sum_banks = ctx.enter_context(tc.psum_pool(name="sum_banks", bufs=4))
 
-        fe_words = keep.tile([P, PASSES, FEATURES], U32, align_bytes=64)
-        fe_planes = keep.tile([P, PASSES, FEATURES], U8, align_bytes=64)
+        fe_words_raw = keep.tile([P, PASSES, FEATURES], U32, align_bytes=64)
+        fe_planes_raw = keep.tile([P, PASSES, FEATURES], U8, align_bytes=64)
+        fe_words = keep.tile([P, PASSES, FEATURE_TILES, P], U32, align_bytes=64)
+        fe_planes = keep.tile([P, PASSES, FEATURE_TILES, P], U8, align_bytes=64)
         fn_words = keep.tile([P, PASSES, FEATURES], U32, align_bytes=64)
         fn_planes = keep.tile([P, PASSES, FEATURES], U8, align_bytes=64)
-        fe_bias_rows = keep.tile([P, P], BF16)
-        nc.vector.memset(fe_planes[:].bitcast(I32), 0)
-        nc.vector.memset(fe_bias_rows[:], 0.0)
+        sums_v = keep.tile([P, FEATURE_TILES, SLOTS, NODES], F32)
+        sums_g = keep.tile([P, len(SHARED_TILES), SLOTS, NODES], F32)
+        nc.vector.memset(fe_planes_raw[:].bitcast(I32), 0)
         nc.vector.memset(fn_planes[:].bitcast(I32), 0)
+        nc.vector.memset(sums_v[:], 0.0)
 
         ident_f32 = keep.tile([P, P], F32)
         make_identity(nc, ident_f32[:])
-        ident_bf16 = keep.tile([P, P], BF16)
-        make_identity(nc, ident_bf16[:])
+        nc.gpsimd.memset(sums_g[:], 0.0)
 
         x_sb = keep.tile([P, FEATURES], BF16)
-        nc.scalar.dma_start(out=fe_bias_rows[0:FEATURE_TILES, :], in_=fe_b2.rearrange("(m p) -> m p", p=P))
+        fe_bias_bf16 = keep.tile([P, FEATURE_TILES], BF16)
+        nc.scalar.dma_start(out=fe_bias_bf16[:], in_=fe_b2.rearrange("(p t) -> p t", t=FEATURE_TILES))
         nc.scalar.dma_start(out=x_sb[:], in_=x_rows)
 
         def load_weight(words_dram, scales_dram, words, planes):
@@ -86,19 +92,17 @@ def tile_graph_gan_pb_kernel(
         e2_tiles = []
         for c in range(CHUNKS):
             tiles = CHUNK_TILES[c]
-            first_row = P * sum(CHUNK_TILES[:c])
+            first_j = sum(CHUNK_TILES[:c])
             e2_sb = e2_pool.tile([P, tiles, EDGE_K], BF16, tag="e2")
             e2_tiles.append(e2_sb)
-            rows = e2_rows[first_row : first_row + P * tiles, :].rearrange("(p a) k -> p a k", a=tiles)
             for a in range(tiles):
-                nc.sync.dma_start(out=e2_sb[:, a, :], in_=rows[:, a, :])
+                nc.sync.dma_start(out=e2_sb[:, a, :], in_=e2_nodes[:, first_j + a, :])
             if c == 0:
-                load_weight(fe_w2_words, fe_w2_scales, fe_words, fe_planes)
+                load_weight(fe_w2_words, fe_w2_scales, fe_words_raw, fe_planes_raw)
         load_weight(fn_w0_words, fn_w0_scales, fn_words, fn_planes)
         fn_bias = keep.tile([P, FEATURES], BF16)
         nc.sync.dma_start(out=fn_bias[:], in_=fn_b0.partition_broadcast(P))
 
-        agg_t = keep.tile([P, FEATURE_TILES, NODES], F32)
         h_codes = keep.tile([P, PASSES, NODES], U32, align_bytes=64)
         h_scales = keep.tile([P, PASSES, NODES], U8, align_bytes=64)
 
@@ -138,13 +142,13 @@ def tile_graph_gan_pb_kernel(
 
         def edge_matmuls(c, codes, scales):
             banks = []
-            for m in range(FEATURE_TILES):
+            for t in range(FEATURE_TILES):
                 edge_sum = sum_banks.tile([P, P * CHUNK_TILES[c]], F32, tag="sums")
                 for g in range(PASSES):
                     nc.tensor.matmul_mx(
                         out=edge_sum[:],
-                        lhsT=fe_words[:, g, P * m : P * (m + 1)].bitcast(FP8X4),
-                        lhsT_scale=fe_planes[:, g, P * m : P * (m + 1)],
+                        lhsT=fe_words[:, g, t, :].bitcast(FP8X4),
+                        lhsT_scale=fe_planes[:, g, t, :],
                         rhs=codes[:, g, :].bitcast(FP8X4),
                         rhs_scale=scales[:, g, :],
                         start=(g == 0),
@@ -153,57 +157,52 @@ def tile_graph_gan_pb_kernel(
                 banks.append(edge_sum)
             return banks
 
-        def scale_sums(c, edge_sums):
-            scaled_tiles = []
-            for m in range(FEATURE_TILES):
-                scaled = scaled_pool.tile([P, P * CHUNK_TILES[c]], F32, tag="scaled")
-                nc.scalar.activation(
-                    out=scaled[:],
-                    in_=edge_sums[m][:],
-                    func=ACT.Identity,
-                    bias=fe_bias_scaled[:, m : m + 1],
-                    scale=SLOPE,
-                )
-                scaled_tiles.append(scaled)
-            return scaled_tiles
+        def relu_on_scalar(c, edge_sums):
+            tiles = {}
+            for t in shared(c):
+                relu = relu_pool.tile([P, P * CHUNK_TILES[c]], F32, tag="relu")
+                nc.scalar.activation(out=relu[:], in_=edge_sums[t][:], func=ACT.Relu, bias=fe_bias[:, t : t + 1], scale=1.0)
+                tiles[t] = relu
+            return tiles
 
-        def leaky_relu(c, edge_sums, scaled_tiles, pair):
-            a3 = stage.tile([P, 2, P * CHUNK_TILES[c]], F32, tag="a3")
-            for i in range(2):
-                m = 2 * pair + i
-                nc.vector.scalar_tensor_tensor(
-                    out=a3[:, i, :],
-                    in0=edge_sums[m][:],
-                    scalar=fe_bias[:, m : m + 1],
-                    in1=scaled_tiles[m][:],
-                    op0=ALU.add,
-                    op1=ALU.max,
-                )
-            if CHUNK_TILES[c] == FOLDED_TILES:
-                kept = slice(P * (FOLDED_TILES - 2), P * (FOLDED_TILES - 1))
-                folded = slice(P * (FOLDED_TILES - 1), P * FOLDED_TILES)
-                nc.gpsimd.tensor_tensor(out=a3[:, :, kept], in0=a3[:, :, kept], in1=a3[:, :, folded], op=ALU.add)
-            return a3
+        def slots_v(c, t):
+            return sums_v[:, t, 0 : CHUNK_TILES[c], :].rearrange("p a n -> p (a n)")
 
-        def sum_neighbours(c, pair, a3):
-            first_node = TILE_NODES * sum(CHUNK_TILES[:c])
-            nodes = TILE_NODES * CHUNK_TILES[c]
-            left = CHUNK_TILES[c] - 1 if CHUNK_TILES[c] == FOLDED_TILES else CHUNK_TILES[c]
-            nc.vector.tensor_reduce(
-                out=agg_t[:, 2 * pair : 2 * pair + 2, first_node : first_node + nodes],
-                in_=a3[:, :, 0 : P * left].rearrange("p m (a n l) -> p m n a l", a=left, n=nodes),
-                axis=AXIS.XY,
-                op=ALU.add,
+        def add_linear(c, edge_sums, t):
+            nc.vector.scalar_tensor_tensor(
+                out=slots_v(c, t), in0=edge_sums[t][:], scalar=0.25, in1=slots_v(c, t), op0=ALU.mult, op1=ALU.add
             )
+
+        def add_clamped(c, edge_sums, t):
+            nc.vector.scalar_tensor_tensor(
+                out=slots_v(c, t),
+                in0=edge_sums[t][:],
+                scalar=fe_bias_negative[:, t : t + 1],
+                in1=slots_v(c, t),
+                op0=ALU.max,
+                op1=ALU.add,
+            )
+
+        def add_relu(c, relu_tiles):
+            for i, t in enumerate(SHARED_TILES):
+                if t in relu_tiles:
+                    slots = sums_g[:, i, 0 : CHUNK_TILES[c], :].rearrange("p a n -> p (a n)")
+                    nc.gpsimd.tensor_tensor(out=slots, in0=slots, in1=relu_tiles[t][:], op=ALU.add)
 
         grouped = regroup_chunk(0, transpose_chunk(0))
 
-        bias_flipped = flip_banks.tile([P, P], BF16, tag="flipped")
-        nc.tensor.transpose(out=bias_flipped[:], in_=fe_bias_rows[:], identity=ident_bf16[:])
         fe_bias = keep.tile([P, FEATURE_TILES], F32)
-        nc.vector.tensor_copy(out=fe_bias[:], in_=bias_flipped[:, 0:FEATURE_TILES])
-        fe_bias_scaled = keep.tile([P, FEATURE_TILES], F32)
-        nc.vector.tensor_scalar_mul(out=fe_bias_scaled[:], in0=fe_bias[:], scalar1=SLOPE)
+        nc.vector.tensor_copy(out=fe_bias[:], in_=fe_bias_bf16[:])
+        fe_bias_negative = keep.tile([P, FEATURE_TILES], F32)
+        nc.vector.tensor_scalar_mul(out=fe_bias_negative[:], in0=fe_bias[:], scalar1=-1.0)
+        fe_bias_start = keep.tile([P, FEATURE_TILES], F32)
+        for t in range(FEATURE_TILES):
+            clamped = sum(CHUNK_TILES[c] for c in range(CHUNKS) if t not in shared(c))
+            nc.vector.tensor_scalar_mul(
+                out=fe_bias_start[:, t : t + 1], in0=fe_bias[:, t : t + 1], scalar1=0.25 * NEIGHBOURS + clamped
+            )
+        for t in range(FEATURE_TILES):
+            nc.vector.tensor_scalar_add(out=sums_v[:, t, 0, :], in0=sums_v[:, t, 1, :], scalar1=fe_bias_start[:, t : t + 1])
 
         x_words = x_sb[:].bitcast(F32)
         x_flipped = flip_banks.tile([P, PAIRS_OF_K, NODES], F32, tag="flipped")
@@ -213,13 +212,18 @@ def tile_graph_gan_pb_kernel(
         nc.scalar.copy(out=x_grouped[:].bitcast(F32), in_=x_flipped[:].rearrange("p u r -> p r u"))
 
         codes, scales = quantise_chunk(0, grouped)
+        for t in range(FEATURE_TILES):
+            nc.vector.tensor_copy(
+                out=fe_words[:, :, t, :].bitcast(I32), in_=fe_words_raw[:].bitcast(I32)[:, :, t:FEATURES:FEATURE_TILES]
+            )
+            nc.vector.tensor_copy(out=fe_planes[:, :, t, :], in_=fe_planes_raw[:, :, t:FEATURES:FEATURE_TILES])
         nc.vector.quantize_mx(
             out=h_codes[:, 1, :].bitcast(FP8X4),
             scales=h_scales[:, 1, :],
             in_=x_grouped[:].rearrange("p r t -> p (r t)"),
         )
 
-        waiting = None
+        live = SLOTS
         for c in range(CHUNKS):
             more = c + 1 < CHUNKS
             if more:
@@ -227,15 +231,41 @@ def tile_graph_gan_pb_kernel(
             edge_sums = edge_matmuls(c, codes, scales)
             if more:
                 grouped = regroup_chunk(c + 1, flipped_banks)
-            scaled_tiles = scale_sums(c, edge_sums)
+            relu_tiles = relu_on_scalar(c, edge_sums)
             if more:
                 codes, scales = quantise_chunk(c + 1, grouped)
-            for pair in range(FEATURE_TILES // 2):
-                a3 = leaky_relu(c, edge_sums, scaled_tiles, pair)
-                if waiting is not None:
-                    sum_neighbours(*waiting)
-                waiting = (c, pair, a3)
-        sum_neighbours(*waiting)
+            previous = None
+            for t in range(FEATURE_TILES):
+                add_linear(c, edge_sums, t)
+                if previous is not None:
+                    add_clamped(c, edge_sums, previous)
+                previous = None if t in relu_tiles else t
+            if previous is not None:
+                add_clamped(c, edge_sums, previous)
+            add_relu(c, relu_tiles)
+            needed = max(CHUNK_TILES[c + 1 :]) if more else 1
+            while live > needed:
+                live //= 2
+                nc.vector.tensor_tensor(
+                    out=sums_v[:, :, 0:live, :], in0=sums_v[:, :, 0:live, :], in1=sums_v[:, :, live : 2 * live, :], op=ALU.add
+                )
+            if c == CHUNKS - VECTOR_ONLY_CHUNKS - 1:
+                width = SLOTS
+                while width > 1:
+                    width //= 2
+                    nc.gpsimd.tensor_tensor(
+                        out=sums_g[:, :, 0:width, :],
+                        in0=sums_g[:, :, 0:width, :],
+                        in1=sums_g[:, :, width : 2 * width, :],
+                        op=ALU.add,
+                    )
+        first_shared = SHARED_TILES[0]
+        nc.vector.tensor_tensor(
+            out=sums_v[:, first_shared:FEATURE_TILES, 0, :],
+            in0=sums_v[:, first_shared:FEATURE_TILES, 0, :],
+            in1=sums_g[:, :, 0, :],
+            op=ALU.add,
+        )
 
         node_sum = sum_banks.tile([P, FEATURES], F32, tag="sums")
 
@@ -252,21 +282,8 @@ def tile_graph_gan_pb_kernel(
 
         node_matmul(1, True, False)
 
-        agg_bf16 = keep.tile([P, FEATURES], BF16)
-        for half in range(2):
-            agg_rows = flip_banks.tile([P, 2, P], F32, tag="flipped")
-            for m in range(2):
-                nc.tensor.transpose(out=agg_rows[:, m, :], in_=agg_t[:, 2 * half + m, :], identity=ident_f32[:])
-            rounded = agg_bf16[:, HALF * half : HALF * (half + 1)]
-            if half == 0:
-                nc.scalar.copy(out=rounded, in_=agg_rows[:].rearrange("p m f -> p (m f)"))
-            else:
-                nc.vector.tensor_copy(out=rounded, in_=agg_rows[:].rearrange("p m f -> p (m f)"))
-        agg_flipped = flip_banks.tile([P, PACK, NODES], BF16, tag="flipped")
-        for t in range(PACK):
-            nc.tensor.transpose(out=agg_flipped[:, t, :], in_=agg_bf16[:, t:FEATURES:PACK], identity=ident_bf16[:])
         agg_grouped = keep.tile([P, NODES, PACK], BF16, align_bytes=64)
-        nc.vector.tensor_copy(out=agg_grouped[:], in_=agg_flipped[:].rearrange("p t r -> p r t"))
+        nc.vector.tensor_scalar_mul(out=agg_grouped[:], in0=sums_v[:, :, 0, :].rearrange("p t n -> p n t"), scalar1=0.8)
         nc.vector.quantize_mx(
             out=h_codes[:, 0, :].bitcast(FP8X4),
             scales=h_scales[:, 0, :],

@@ -30,7 +30,7 @@ CHUNKS = len(CHUNK_TILES)
 SLOTS = 4
 assert sum(CHUNK_TILES) == NEIGHBOURS
 VECTOR_ONLY_CHUNKS = 1
-SHARED_TILES = [1, 2, 3]
+SHARED_TILES = [2, 3]
 HALF = FEATURES // 2
 SLOPE = 0.2
 

@@ -28,7 +28,9 @@ FEATURE_TILES = FEATURES // P
 CHUNK_TILES = [2, 2] + [4] * 6 + [2, 2]
 CHUNKS = len(CHUNK_TILES)
 SLOTS = 4
+G_SLOTS = 2
 assert sum(CHUNK_TILES) == NEIGHBOURS
+LAST_FULL = max(c for c in range(CHUNKS) if CHUNK_TILES[c] > 2)
 VECTOR_ONLY_CHUNKS = 1
 SHARED_TILES = [2, 3]
 HALF = FEATURES // 2
@@ -64,7 +66,7 @@ def tile_graph_gan_pb_kernel(
         fn_words = keep.tile([P, PASSES, FEATURES], U32, align_bytes=64)
         fn_planes = keep.tile([P, PASSES, FEATURES], U8, align_bytes=64)
         sums_v = keep.tile([P, FEATURE_TILES, SLOTS, NODES], F32)
-        sums_g = keep.tile([P, len(SHARED_TILES), SLOTS, NODES], F32)
+        sums_g = keep.tile([P, len(SHARED_TILES), G_SLOTS, NODES], F32)
         nc.vector.memset(fe_planes_raw[:].bitcast(I32), 0)
         nc.vector.memset(fn_planes[:].bitcast(I32), 0)
         nc.vector.memset(sums_v[:], 0.0)
@@ -184,13 +186,19 @@ def tile_graph_gan_pb_kernel(
             )
 
         def add_relu(c, relu_tiles):
-            for i, t in enumerate(SHARED_TILES):
-                if t in relu_tiles:
-                    slots = sums_g[:, i, 0 : CHUNK_TILES[c], :].rearrange("p a n -> p (a n)")
-                    nc.gpsimd.tensor_tensor(out=slots, in0=slots, in1=relu_tiles[t][:], op=ALU.add)
+            width = G_SLOTS * NODES
+            for piece in range(CHUNK_TILES[c] // G_SLOTS):
+                for i, t in enumerate(SHARED_TILES):
+                    if t in relu_tiles:
+                        slots = sums_g[:, i, :, :].rearrange("p a n -> p (a n)")
+                        nc.gpsimd.tensor_tensor(
+                            out=slots, in0=slots, in1=relu_tiles[t][:, width * piece : width * (piece + 1)], op=ALU.add
+                        )
 
         grouped = regroup_chunk(0, transpose_chunk(0))
 
+        ident_scaled = keep.tile([P, P], F32)
+        nc.vector.tensor_scalar_mul(out=ident_scaled[:], in0=ident_f32[:], scalar1=0.8)
         fe_bias = keep.tile([P, FEATURE_TILES], F32)
         nc.vector.tensor_copy(out=fe_bias[:], in_=fe_bias_bf16[:])
         fe_bias_negative = keep.tile([P, FEATURE_TILES], F32)
@@ -223,7 +231,7 @@ def tile_graph_gan_pb_kernel(
             in_=x_grouped[:].rearrange("p r t -> p (r t)"),
         )
 
-        live = SLOTS
+        first_shared = SHARED_TILES[0]
         for c in range(CHUNKS):
             more = c + 1 < CHUNKS
             if more:
@@ -243,29 +251,15 @@ def tile_graph_gan_pb_kernel(
             if previous is not None:
                 add_clamped(c, edge_sums, previous)
             add_relu(c, relu_tiles)
-            needed = max(CHUNK_TILES[c + 1 :]) if more else 1
-            while live > needed:
-                live //= 2
-                nc.vector.tensor_tensor(
-                    out=sums_v[:, :, 0:live, :], in0=sums_v[:, :, 0:live, :], in1=sums_v[:, :, live : 2 * live, :], op=ALU.add
-                )
             if c == CHUNKS - VECTOR_ONLY_CHUNKS - 1:
-                width = SLOTS
-                while width > 1:
-                    width //= 2
-                    nc.gpsimd.tensor_tensor(
-                        out=sums_g[:, :, 0:width, :],
-                        in0=sums_g[:, :, 0:width, :],
-                        in1=sums_g[:, :, width : 2 * width, :],
-                        op=ALU.add,
-                    )
-        first_shared = SHARED_TILES[0]
-        nc.vector.tensor_tensor(
-            out=sums_v[:, first_shared:FEATURE_TILES, 0, :],
-            in0=sums_v[:, first_shared:FEATURE_TILES, 0, :],
-            in1=sums_g[:, :, 0, :],
-            op=ALU.add,
-        )
+                nc.gpsimd.tensor_tensor(out=sums_g[:, :, 0, :], in0=sums_g[:, :, 0, :], in1=sums_g[:, :, 1, :], op=ALU.add)
+                nc.gpsimd.tensor_tensor(
+                    out=sums_v[:, first_shared:FEATURE_TILES, 2, :],
+                    in0=sums_v[:, first_shared:FEATURE_TILES, 2, :],
+                    in1=sums_g[:, :, 0, :],
+                    op=ALU.add,
+                )
+        nc.vector.tensor_tensor(out=sums_v[:, :, 0, :], in0=sums_v[:, :, 0, :], in1=sums_v[:, :, 1, :], op=ALU.add)
 
         node_sum = sum_banks.tile([P, FEATURES], F32, tag="sums")
 
@@ -282,8 +276,19 @@ def tile_graph_gan_pb_kernel(
 
         node_matmul(1, True, False)
 
+        folded = flip_banks.tile([P, FEATURE_TILES, NODES], F32, tag="flipped")
+        for a in (3, 2):
+            nc.tensor.matmul(out=folded[:], lhsT=ident_scaled[:], rhs=sums_v[:, :, a, :], start=(a == 3), stop=(a == 2))
+
         agg_grouped = keep.tile([P, NODES, PACK], BF16, align_bytes=64)
-        nc.vector.tensor_scalar_mul(out=agg_grouped[:], in0=sums_v[:, :, 0, :].rearrange("p t n -> p n t"), scalar1=0.8)
+        nc.vector.scalar_tensor_tensor(
+            out=agg_grouped[:],
+            in0=sums_v[:, :, 0, :].rearrange("p t n -> p n t"),
+            scalar=0.8,
+            in1=folded[:].rearrange("p t n -> p n t"),
+            op0=ALU.mult,
+            op1=ALU.add,
+        )
         nc.vector.quantize_mx(
             out=h_codes[:, 0, :].bitcast(FP8X4),
             scales=h_scales[:, 0, :],

@@ -47,6 +47,9 @@ def tile_graph_gan_pb_kernel(
     x_rows = x.rearrange("b i d -> (b i) d")
     out_rows = out.rearrange("b i f -> (b i) f")
 
+    def tiles_in_bank(c):
+        return SLOTS // CHUNK_TILES[c]
+
     def shared(c):
         return SHARED_TILES if c < CHUNKS - VECTOR_ONLY_CHUNKS else []
 
@@ -67,6 +70,9 @@ def tile_graph_gan_pb_kernel(
         fn_planes = keep.tile([P, PASSES, FEATURES], U8, align_bytes=64)
         sums_v = keep.tile([P, FEATURE_TILES, SLOTS, NODES], F32)
         sums_g = keep.tile([P, len(SHARED_TILES), G_SLOTS, NODES], F32)
+        warm = keep.tile([P, 2], F32)
+        nc.vector.memset(warm[:], 0.0)
+        nc.scalar.activation(out=warm[:, 1:2], in_=warm[:, 0:1], func=ACT.Relu)
         nc.vector.memset(fe_planes_raw[:].bitcast(I32), 0)
         nc.vector.memset(fn_planes[:].bitcast(I32), 0)
         nc.vector.memset(sums_v[:], 0.0)
@@ -143,42 +149,45 @@ def tile_graph_gan_pb_kernel(
             return codes, scales
 
         def edge_matmuls(c, codes, scales):
-            banks = []
-            for t in range(FEATURE_TILES):
-                edge_sum = sum_banks.tile([P, P * CHUNK_TILES[c]], F32, tag="sums")
-                for g in range(PASSES):
-                    nc.tensor.matmul_mx(
-                        out=edge_sum[:],
-                        lhsT=fe_words[:, g, t, :].bitcast(FP8X4),
-                        lhsT_scale=fe_planes[:, g, t, :],
-                        rhs=codes[:, g, :].bitcast(FP8X4),
-                        rhs_scale=scales[:, g, :],
-                        start=(g == 0),
-                        stop=(g == PASSES - 1),
-                    )
-                banks.append(edge_sum)
-            return banks
+            banks, edge_sums = [], []
+            for first in range(0, FEATURE_TILES, tiles_in_bank(c)):
+                bank = sum_banks.tile([P, tiles_in_bank(c), P * CHUNK_TILES[c]], F32, tag="sums")
+                banks.append(bank)
+                for i in range(tiles_in_bank(c)):
+                    t = first + i
+                    for g in range(PASSES):
+                        nc.tensor.matmul_mx(
+                            out=bank[:, i, :],
+                            lhsT=fe_words[:, g, t, :].bitcast(FP8X4),
+                            lhsT_scale=fe_planes[:, g, t, :],
+                            rhs=codes[:, g, :].bitcast(FP8X4),
+                            rhs_scale=scales[:, g, :],
+                            start=(g == 0),
+                            stop=(g == PASSES - 1),
+                        )
+                    edge_sums.append(bank[:, i, :])
+            return banks, edge_sums
 
         def relu_on_scalar(c, edge_sums):
             tiles = {}
             for t in shared(c):
                 relu = relu_pool.tile([P, P * CHUNK_TILES[c]], F32, tag="relu")
-                nc.scalar.activation(out=relu[:], in_=edge_sums[t][:], func=ACT.Relu, bias=fe_bias[:, t : t + 1], scale=1.0)
+                nc.scalar.activation(out=relu[:], in_=edge_sums[t], func=ACT.Relu, bias=fe_bias[:, t : t + 1], scale=1.0)
                 tiles[t] = relu
             return tiles
 
         def slots_v(c, t):
             return sums_v[:, t, 0 : CHUNK_TILES[c], :].rearrange("p a n -> p (a n)")
 
-        def add_linear(c, edge_sums, t):
-            nc.vector.scalar_tensor_tensor(
-                out=slots_v(c, t), in0=edge_sums[t][:], scalar=0.25, in1=slots_v(c, t), op0=ALU.mult, op1=ALU.add
-            )
+        def add_linear(c, banks, k):
+            first = k * tiles_in_bank(c)
+            slots = sums_v[:, first : first + tiles_in_bank(c), 0 : CHUNK_TILES[c], :].rearrange("p t a n -> p t (a n)")
+            nc.vector.scalar_tensor_tensor(out=slots, in0=banks[k][:], scalar=0.25, in1=slots, op0=ALU.mult, op1=ALU.add)
 
         def add_clamped(c, edge_sums, t):
             nc.vector.scalar_tensor_tensor(
                 out=slots_v(c, t),
-                in0=edge_sums[t][:],
+                in0=edge_sums[t],
                 scalar=fe_bias_negative[:, t : t + 1],
                 in1=slots_v(c, t),
                 op0=ALU.max,
@@ -236,20 +245,20 @@ def tile_graph_gan_pb_kernel(
             more = c + 1 < CHUNKS
             if more:
                 flipped_banks = transpose_chunk(c + 1)
-            edge_sums = edge_matmuls(c, codes, scales)
+            banks, edge_sums = edge_matmuls(c, codes, scales)
             if more:
                 grouped = regroup_chunk(c + 1, flipped_banks)
             relu_tiles = relu_on_scalar(c, edge_sums)
             if more:
                 codes, scales = quantise_chunk(c + 1, grouped)
-            previous = None
-            for t in range(FEATURE_TILES):
-                add_linear(c, edge_sums, t)
-                if previous is not None:
-                    add_clamped(c, edge_sums, previous)
-                previous = None if t in relu_tiles else t
-            if previous is not None:
-                add_clamped(c, edge_sums, previous)
+            previous = []
+            for k in range(len(banks)):
+                add_linear(c, banks, k)
+                for t in previous:
+                    add_clamped(c, edge_sums, t)
+                previous = [t for t in range(k * tiles_in_bank(c), (k + 1) * tiles_in_bank(c)) if t not in relu_tiles]
+            for t in previous:
+                add_clamped(c, edge_sums, t)
             add_relu(c, relu_tiles)
             if c == CHUNKS - VECTOR_ONLY_CHUNKS - 1:
                 nc.gpsimd.tensor_tensor(out=sums_g[:, :, 0, :], in0=sums_g[:, :, 0, :], in1=sums_g[:, :, 1, :], op=ALU.add)

@@ -25,12 +25,13 @@ EDGE_K = 1024
 FEATURES = 512
 FEATURE_TILES = FEATURES // P
 
-CHUNK_TILES = [2, 2] + [4] * 6 + [2, 2]
+CHUNK_TILES = [2] + [4] * 7 + [2]
 CHUNKS = len(CHUNK_TILES)
 SLOTS = 4
 G_SLOTS = 2
 assert sum(CHUNK_TILES) == NEIGHBOURS
 LAST_FULL = max(c for c in range(CHUNKS) if CHUNK_TILES[c] > 2)
+X_ROUND = LAST_FULL
 VECTOR_ONLY_CHUNKS = 1
 SHARED_TILES = [2, 3]
 HALF = FEATURES // 2
@@ -84,7 +85,6 @@ def tile_graph_gan_pb_kernel(
         x_sb = keep.tile([P, FEATURES], BF16)
         fe_bias_bf16 = keep.tile([P, FEATURE_TILES], BF16)
         nc.scalar.dma_start(out=fe_bias_bf16[:], in_=fe_b2.rearrange("(p t) -> p t", t=FEATURE_TILES))
-        nc.scalar.dma_start(out=x_sb[:], in_=x_rows)
 
         def load_weight(words_dram, scales_dram, words, planes):
             for quadrant in range(4):
@@ -107,6 +107,8 @@ def tile_graph_gan_pb_kernel(
                 nc.sync.dma_start(out=e2_sb[:, a, :], in_=e2_nodes[:, first_j + a, :])
             if c == 0:
                 load_weight(fe_w2_words, fe_w2_scales, fe_words_raw, fe_planes_raw)
+            if c == X_ROUND - 2:
+                nc.sync.dma_start(out=x_sb[:], in_=x_rows)
         load_weight(fn_w0_words, fn_w0_scales, fn_words, fn_planes)
         fn_bias = keep.tile([P, FEATURES], BF16)
         nc.sync.dma_start(out=fn_bias[:], in_=fn_b0.partition_broadcast(P))
@@ -221,36 +223,38 @@ def tile_graph_gan_pb_kernel(
         for t in range(FEATURE_TILES):
             nc.vector.tensor_scalar_add(out=sums_v[:, t, 0, :], in0=sums_v[:, t, 1, :], scalar1=fe_bias_start[:, t : t + 1])
 
-        x_words = x_sb[:].bitcast(F32)
-        x_flipped = flip_banks.tile([P, PAIRS_OF_K, NODES], F32, tag="flipped")
-        for u in range(PAIRS_OF_K):
-            nc.tensor.transpose(out=x_flipped[:, u, :], in_=x_words[:, u:WORDS:PAIRS_OF_K], identity=ident_f32[:])
-        x_grouped = keep.tile([P, NODES, PACK], BF16, align_bytes=64)
-        nc.scalar.copy(out=x_grouped[:].bitcast(F32), in_=x_flipped[:].rearrange("p u r -> p r u"))
-
         codes, scales = quantise_chunk(0, grouped)
         for t in range(FEATURE_TILES):
             nc.vector.tensor_copy(
                 out=fe_words[:, :, t, :].bitcast(I32), in_=fe_words_raw[:].bitcast(I32)[:, :, t:FEATURES:FEATURE_TILES]
             )
             nc.vector.tensor_copy(out=fe_planes[:, :, t, :], in_=fe_planes_raw[:, :, t:FEATURES:FEATURE_TILES])
-        nc.vector.quantize_mx(
-            out=h_codes[:, 1, :].bitcast(FP8X4),
-            scales=h_scales[:, 1, :],
-            in_=x_grouped[:].rearrange("p r t -> p (r t)"),
-        )
+        x_grouped = keep.tile([P, NODES, PACK], BF16, align_bytes=64)
 
         first_shared = SHARED_TILES[0]
         for c in range(CHUNKS):
             more = c + 1 < CHUNKS
             if more:
                 flipped_banks = transpose_chunk(c + 1)
+            if c == X_ROUND:
+                x_words = x_sb[:].bitcast(F32)
+                x_flipped = flip_banks.tile([P, PAIRS_OF_K, NODES], F32, tag="flipped")
+                for u in range(PAIRS_OF_K):
+                    nc.tensor.transpose(out=x_flipped[:, u, :], in_=x_words[:, u:WORDS:PAIRS_OF_K], identity=ident_f32[:])
             banks, edge_sums = edge_matmuls(c, codes, scales)
             if more:
                 grouped = regroup_chunk(c + 1, flipped_banks)
+            if c == X_ROUND:
+                nc.scalar.copy(out=x_grouped[:].bitcast(F32), in_=x_flipped[:].rearrange("p u r -> p r u"))
             relu_tiles = relu_on_scalar(c, edge_sums)
             if more:
                 codes, scales = quantise_chunk(c + 1, grouped)
+            if c == X_ROUND:
+                nc.vector.quantize_mx(
+                    out=h_codes[:, 1, :].bitcast(FP8X4),
+                    scales=h_scales[:, 1, :],
+                    in_=x_grouped[:].rearrange("p r t -> p (r t)"),
+                )
             previous = []
             for k in range(len(banks)):
                 add_linear(c, banks, k)

@@ -71,6 +71,8 @@ def tile_graph_gan_pb_kernel(
         fn_planes = keep.tile([P, PASSES, FEATURES], U8, align_bytes=64)
         sums_v = keep.tile([P, FEATURE_TILES, SLOTS, NODES], F32)
         sums_g = keep.tile([P, len(SHARED_TILES), G_SLOTS, NODES], F32)
+        fe_bias_bf16 = keep.tile([P, FEATURE_TILES], BF16)
+        nc.scalar.dma_start(out=fe_bias_bf16[:], in_=fe_b2.rearrange("(p t) -> p t", t=FEATURE_TILES))
         warm = keep.tile([P, 2], F32)
         nc.vector.memset(warm[:], 0.0)
         nc.scalar.activation(out=warm[:, 1:2], in_=warm[:, 0:1], func=ACT.Relu)
@@ -83,8 +85,6 @@ def tile_graph_gan_pb_kernel(
         nc.gpsimd.memset(sums_g[:], 0.0)
 
         x_sb = keep.tile([P, FEATURES], BF16)
-        fe_bias_bf16 = keep.tile([P, FEATURE_TILES], BF16)
-        nc.scalar.dma_start(out=fe_bias_bf16[:], in_=fe_b2.rearrange("(p t) -> p t", t=FEATURE_TILES))
 
         def load_weight(words_dram, scales_dram, words, planes):
             for quadrant in range(4):

@@ -33,7 +33,7 @@ assert sum(CHUNK_TILES) == NEIGHBOURS
 LAST_FULL = max(c for c in range(CHUNKS) if CHUNK_TILES[c] > 2)
 X_ROUND = LAST_FULL
 VECTOR_ONLY_CHUNKS = 1
-SHARED_TILES = [2, 3]
+SHARED_TILES = [0, 1]
 HALF = FEATURES // 2
 SLOPE = 0.2
 
@@ -267,8 +267,8 @@ def tile_graph_gan_pb_kernel(
             if c == CHUNKS - VECTOR_ONLY_CHUNKS - 1:
                 nc.gpsimd.tensor_tensor(out=sums_g[:, :, 0, :], in0=sums_g[:, :, 0, :], in1=sums_g[:, :, 1, :], op=ALU.add)
                 nc.gpsimd.tensor_tensor(
-                    out=sums_v[:, first_shared:FEATURE_TILES, 2, :],
-                    in0=sums_v[:, first_shared:FEATURE_TILES, 2, :],
+                    out=sums_v[:, first_shared : first_shared + len(SHARED_TILES), 2, :],
+                    in0=sums_v[:, first_shared : first_shared + len(SHARED_TILES), 2, :],
                     in1=sums_g[:, :, 0, :],
                     op=ALU.add,
                 )

@@ -30,10 +30,9 @@ CHUNKS = len(CHUNK_TILES)
 SLOTS = 4
 G_SLOTS = 2
 assert sum(CHUNK_TILES) == NEIGHBOURS
-LAST_FULL = max(c for c in range(CHUNKS) if CHUNK_TILES[c] > 2)
-X_ROUND = LAST_FULL
-VECTOR_ONLY_CHUNKS = 1
+X_LOAD = CHUNKS - 4
 SHARED_TILES = [0, 1]
+LATE_TILES = {CHUNKS - 2: [2], CHUNKS - 1: [0, 1, 2, 3]}
 HALF = FEATURES // 2
 SLOPE = 0.2
 
@@ -52,7 +51,10 @@ def tile_graph_gan_pb_kernel(
         return SLOTS // CHUNK_TILES[c]
 
     def shared(c):
-        return SHARED_TILES if c < CHUNKS - VECTOR_ONLY_CHUNKS else []
+        return SHARED_TILES if c < CHUNKS - 1 else []
+
+    def late(c):
+        return LATE_TILES.get(c, [])
 
     with ExitStack() as ctx:
         ctx.enter_context(tc.manual_schedule())
@@ -60,28 +62,30 @@ def tile_graph_gan_pb_kernel(
         e2_pool = ctx.enter_context(tc.tile_pool(name="e2", bufs=CHUNKS))
         stage = ctx.enter_context(tc.tile_pool(name="stage", bufs=2))
         relu_pool = ctx.enter_context(tc.tile_pool(name="relu", bufs=2 * len(SHARED_TILES)))
+        late_pool = ctx.enter_context(tc.tile_pool(name="late", bufs=sum(len(tiles) for tiles in LATE_TILES.values())))
         flip_banks = ctx.enter_context(tc.psum_pool(name="flip_banks", bufs=4))
         sum_banks = ctx.enter_context(tc.psum_pool(name="sum_banks", bufs=4))
 
-        fe_words_raw = keep.tile([P, PASSES, FEATURES], U32, align_bytes=64)
-        fe_planes_raw = keep.tile([P, PASSES, FEATURES], U8, align_bytes=64)
-        fe_words = keep.tile([P, PASSES, FEATURE_TILES, P], U32, align_bytes=64)
-        fe_planes = keep.tile([P, PASSES, FEATURE_TILES, P], U8, align_bytes=64)
+        fe_words = keep.tile([P, PASSES, FEATURES], U32, align_bytes=64)
+        fe_planes = keep.tile([P, PASSES, FEATURES], U8, align_bytes=64)
         fn_words = keep.tile([P, PASSES, FEATURES], U32, align_bytes=64)
         fn_planes = keep.tile([P, PASSES, FEATURES], U8, align_bytes=64)
         sums_v = keep.tile([P, FEATURE_TILES, SLOTS, NODES], F32)
         sums_g = keep.tile([P, len(SHARED_TILES), G_SLOTS, NODES], F32)
-        fe_bias_bf16 = keep.tile([P, FEATURE_TILES], BF16)
-        nc.scalar.dma_start(out=fe_bias_bf16[:], in_=fe_b2.rearrange("(p t) -> p t", t=FEATURE_TILES))
+        fe_bias_rows = keep.tile([P, P], BF16, align_bytes=64)
+        nc.vector.memset(fe_bias_rows[:], 0.0)
+        nc.scalar.dma_start(out=fe_bias_rows[0:FEATURE_TILES, :], in_=fe_b2.rearrange("(t p) -> t p", t=FEATURE_TILES))
         warm = keep.tile([P, 2], F32)
         nc.vector.memset(warm[:], 0.0)
         nc.scalar.activation(out=warm[:, 1:2], in_=warm[:, 0:1], func=ACT.Relu)
-        nc.vector.memset(fe_planes_raw[:].bitcast(I32), 0)
+        nc.vector.memset(fe_planes[:].bitcast(I32), 0)
         nc.vector.memset(fn_planes[:].bitcast(I32), 0)
         nc.vector.memset(sums_v[:], 0.0)
 
         ident_f32 = keep.tile([P, P], F32)
         make_identity(nc, ident_f32[:])
+        ident_bf16 = keep.tile([P, P], BF16, align_bytes=64)
+        nc.gpsimd.tensor_copy(out=ident_bf16[:], in_=ident_f32[:])
         nc.gpsimd.memset(sums_g[:], 0.0)
 
         x_sb = keep.tile([P, FEATURES], BF16)
@@ -106,8 +110,8 @@ def tile_graph_gan_pb_kernel(
             for a in range(tiles):
                 nc.sync.dma_start(out=e2_sb[:, a, :], in_=e2_nodes[:, first_j + a, :])
             if c == 0:
-                load_weight(fe_w2_words, fe_w2_scales, fe_words_raw, fe_planes_raw)
-            if c == X_ROUND - 2:
+                load_weight(fe_w2_words, fe_w2_scales, fe_words, fe_planes)
+            if c == X_LOAD:
                 nc.sync.dma_start(out=x_sb[:], in_=x_rows)
         load_weight(fn_w0_words, fn_w0_scales, fn_words, fn_planes)
         fn_bias = keep.tile([P, FEATURES], BF16)
@@ -160,8 +164,8 @@ def tile_graph_gan_pb_kernel(
                     for g in range(PASSES):
                         nc.tensor.matmul_mx(
                             out=bank[:, i, :],
-                            lhsT=fe_words[:, g, t, :].bitcast(FP8X4),
-                            lhsT_scale=fe_planes[:, g, t, :],
+                            lhsT=fe_words[:, g, P * t : P * (t + 1)].bitcast(FP8X4),
+                            lhsT_scale=fe_planes[:, g, P * t : P * (t + 1)],
                             rhs=codes[:, g, :].bitcast(FP8X4),
                             rhs_scale=scales[:, g, :],
                             start=(g == 0),
@@ -172,8 +176,11 @@ def tile_graph_gan_pb_kernel(
 
         def relu_on_scalar(c, edge_sums):
             tiles = {}
-            for t in shared(c):
-                relu = relu_pool.tile([P, P * CHUNK_TILES[c]], F32, tag="relu")
+            for t in shared(c) + late(c):
+                if t in shared(c):
+                    relu = relu_pool.tile([P, P * CHUNK_TILES[c]], F32, tag="relu")
+                else:
+                    relu = late_pool.tile([P, P * CHUNK_TILES[c]], F32, tag="late")
                 nc.scalar.activation(out=relu[:], in_=edge_sums[t], func=ACT.Relu, bias=fe_bias[:, t : t + 1], scale=1.0)
                 tiles[t] = relu
             return tiles
@@ -208,53 +215,36 @@ def tile_graph_gan_pb_kernel(
 
         grouped = regroup_chunk(0, transpose_chunk(0))
 
-        ident_scaled = keep.tile([P, P], F32)
-        nc.vector.tensor_scalar_mul(out=ident_scaled[:], in0=ident_f32[:], scalar1=0.8)
+        codes, scales = quantise_chunk(0, grouped)
+
+        bias_flipped = flip_banks.tile([P, P], BF16, tag="flipped")
+        nc.tensor.transpose(out=bias_flipped[:], in_=fe_bias_rows[:], identity=ident_bf16[:])
         fe_bias = keep.tile([P, FEATURE_TILES], F32)
-        nc.vector.tensor_copy(out=fe_bias[:], in_=fe_bias_bf16[:])
+        nc.vector.tensor_copy(out=fe_bias[:], in_=bias_flipped[:, 0:FEATURE_TILES])
         fe_bias_negative = keep.tile([P, FEATURE_TILES], F32)
         nc.vector.tensor_scalar_mul(out=fe_bias_negative[:], in0=fe_bias[:], scalar1=-1.0)
         fe_bias_start = keep.tile([P, FEATURE_TILES], F32)
         for t in range(FEATURE_TILES):
-            clamped = sum(CHUNK_TILES[c] for c in range(CHUNKS) if t not in shared(c))
+            clamped = sum(CHUNK_TILES[c] for c in range(CHUNKS) if t not in shared(c) + late(c))
             nc.vector.tensor_scalar_mul(
                 out=fe_bias_start[:, t : t + 1], in0=fe_bias[:, t : t + 1], scalar1=0.25 * NEIGHBOURS + clamped
             )
         for t in range(FEATURE_TILES):
             nc.vector.tensor_scalar_add(out=sums_v[:, t, 0, :], in0=sums_v[:, t, 1, :], scalar1=fe_bias_start[:, t : t + 1])
 
-        codes, scales = quantise_chunk(0, grouped)
-        for t in range(FEATURE_TILES):
-            nc.vector.tensor_copy(
-                out=fe_words[:, :, t, :].bitcast(I32), in_=fe_words_raw[:].bitcast(I32)[:, :, t:FEATURES:FEATURE_TILES]
-            )
-            nc.vector.tensor_copy(out=fe_planes[:, :, t, :], in_=fe_planes_raw[:, :, t:FEATURES:FEATURE_TILES])
         x_grouped = keep.tile([P, NODES, PACK], BF16, align_bytes=64)
 
-        first_shared = SHARED_TILES[0]
+        late_relus = []
         for c in range(CHUNKS):
             more = c + 1 < CHUNKS
             if more:
                 flipped_banks = transpose_chunk(c + 1)
-            if c == X_ROUND:
-                x_words = x_sb[:].bitcast(F32)
-                x_flipped = flip_banks.tile([P, PAIRS_OF_K, NODES], F32, tag="flipped")
-                for u in range(PAIRS_OF_K):
-                    nc.tensor.transpose(out=x_flipped[:, u, :], in_=x_words[:, u:WORDS:PAIRS_OF_K], identity=ident_f32[:])
             banks, edge_sums = edge_matmuls(c, codes, scales)
             if more:
                 grouped = regroup_chunk(c + 1, flipped_banks)
-            if c == X_ROUND:
-                nc.scalar.copy(out=x_grouped[:].bitcast(F32), in_=x_flipped[:].rearrange("p u r -> p r u"))
             relu_tiles = relu_on_scalar(c, edge_sums)
             if more:
                 codes, scales = quantise_chunk(c + 1, grouped)
-            if c == X_ROUND:
-                nc.vector.quantize_mx(
-                    out=h_codes[:, 1, :].bitcast(FP8X4),
-                    scales=h_scales[:, 1, :],
-                    in_=x_grouped[:].rearrange("p r t -> p (r t)"),
-                )
             previous = []
             for k in range(len(banks)):
                 add_linear(c, banks, k)
@@ -263,16 +253,44 @@ def tile_graph_gan_pb_kernel(
                 previous = [t for t in range(k * tiles_in_bank(c), (k + 1) * tiles_in_bank(c)) if t not in relu_tiles]
             for t in previous:
                 add_clamped(c, edge_sums, t)
-            add_relu(c, relu_tiles)
-            if c == CHUNKS - VECTOR_ONLY_CHUNKS - 1:
-                nc.gpsimd.tensor_tensor(out=sums_g[:, :, 0, :], in0=sums_g[:, :, 0, :], in1=sums_g[:, :, 1, :], op=ALU.add)
-                nc.gpsimd.tensor_tensor(
-                    out=sums_v[:, first_shared : first_shared + len(SHARED_TILES), 2, :],
-                    in0=sums_v[:, first_shared : first_shared + len(SHARED_TILES), 2, :],
-                    in1=sums_g[:, :, 0, :],
-                    op=ALU.add,
-                )
-        nc.vector.tensor_tensor(out=sums_v[:, :, 0, :], in0=sums_v[:, :, 0, :], in1=sums_v[:, :, 1, :], op=ALU.add)
+            add_relu(c, {t: relu_tiles[t] for t in shared(c)})
+            late_relus += [(t, relu_tiles[t], a) for t in late(c) for a in range(CHUNK_TILES[c])]
+
+        def flip_row(row_words):
+            flipped = flip_banks.tile([P, PAIRS_OF_K, NODES], F32, tag="flipped")
+            for u in range(PAIRS_OF_K):
+                nc.tensor.transpose(out=flipped[:, u, :], in_=row_words[:, u:WORDS:PAIRS_OF_K], identity=ident_f32[:])
+            return flipped
+
+        def quantise_half(g, grouped_half):
+            nc.vector.quantize_mx(
+                out=h_codes[:, g, :].bitcast(FP8X4),
+                scales=h_scales[:, g, :],
+                in_=grouped_half[:].rearrange("p r t -> p (r t)"),
+            )
+
+        x_flipped = flip_row(x_sb[:].bitcast(F32))
+        nc.scalar.copy(out=x_grouped[:].bitcast(F32), in_=x_flipped[:].rearrange("p u r -> p r u"))
+        quantise_half(1, x_grouped)
+
+        parts = [(t, relu, slice(P * a, P * (a + 1))) for t, relu, a in late_relus]
+        pieces = [(t, relu[:, cols]) for t, relu, cols in parts]
+        pieces += [(t, sums_v[:, t, a, :]) for a in (3, 2) for t in range(FEATURE_TILES)]
+        pieces += [(t, sums_g[:, i, a, :]) for i, t in enumerate(SHARED_TILES) for a in range(G_SLOTS)]
+        pieces += [(t, sums_v[:, t, a, :]) for a in (0, 1) for t in range(FEATURE_TILES)]
+        agg_banks = []
+        for t in range(FEATURE_TILES):
+            agg_bank = flip_banks.tile([P, P], F32, tag="flipped")
+            agg_banks.append(agg_bank)
+        for i, (t, piece) in enumerate(pieces):
+            nc.tensor.matmul(
+                out=agg_banks[t][:],
+                lhsT=piece,
+                rhs=ident_f32[:],
+                is_transpose=True,
+                start=t not in [other for other, _ in pieces[:i]],
+                stop=t not in [other for other, _ in pieces[i + 1 :]],
+            )
 
         node_sum = sum_banks.tile([P, FEATURES], F32, tag="sums")
 
@@ -289,24 +307,17 @@ def tile_graph_gan_pb_kernel(
 
         node_matmul(1, True, False)
 
-        folded = flip_banks.tile([P, FEATURE_TILES, NODES], F32, tag="flipped")
-        for a in (3, 2):
-            nc.tensor.matmul(out=folded[:], lhsT=ident_scaled[:], rhs=sums_v[:, :, a, :], start=(a == 3), stop=(a == 2))
-
+        agg_sb = keep.tile([P, FEATURES], BF16)
+        for t in range(FEATURE_TILES):
+            cols = slice(P * t, P * (t + 1))
+            if t % 2 == 0:
+                nc.scalar.activation(out=agg_sb[:, cols], in_=agg_banks[t][:], func=ACT.Copy, scale=0.8)
+            else:
+                nc.vector.tensor_scalar_mul(out=agg_sb[:, cols], in0=agg_banks[t][:], scalar1=0.8)
+        agg_flipped = flip_row(agg_sb[:].bitcast(F32))
         agg_grouped = keep.tile([P, NODES, PACK], BF16, align_bytes=64)
-        nc.vector.scalar_tensor_tensor(
-            out=agg_grouped[:],
-            in0=sums_v[:, :, 0, :].rearrange("p t n -> p n t"),
-            scalar=0.8,
-            in1=folded[:].rearrange("p t n -> p n t"),
-            op0=ALU.mult,
-            op1=ALU.add,
-        )
-        nc.vector.quantize_mx(
-            out=h_codes[:, 0, :].bitcast(FP8X4),
-            scales=h_scales[:, 0, :],
-            in_=agg_grouped[:].rearrange("p r t -> p (r t)"),
-        )
+        nc.scalar.copy(out=agg_grouped[:].bitcast(F32), in_=agg_flipped[:].rearrange("p u r -> p r u"))
+        quantise_half(0, agg_grouped)
         node_matmul(0, False, True)
 
         biased = keep.tile([P, FEATURES], F32)

@@ -254,10 +254,10 @@ def tile_graph_gan_pb_kernel(
             for t in previous:
                 add_clamped(c, edge_sums, t)
             add_relu(c, {t: relu_tiles[t] for t in shared(c)})
-            late_relus += [(t, relu_tiles[t], a) for t in late(c) for a in range(CHUNK_TILES[c])]
+            late_relus += [(c, t, relu_tiles[t][:, P * a : P * (a + 1)]) for t in late(c) for a in range(CHUNK_TILES[c])]
 
         def flip_row(row_words):
-            flipped = flip_banks.tile([P, PAIRS_OF_K, NODES], F32, tag="flipped")
+            flipped = sum_banks.tile([P, PAIRS_OF_K, NODES], F32, tag="sums")
             for u in range(PAIRS_OF_K):
                 nc.tensor.transpose(out=flipped[:, u, :], in_=row_words[:, u:WORDS:PAIRS_OF_K], identity=ident_f32[:])
             return flipped
@@ -269,15 +269,11 @@ def tile_graph_gan_pb_kernel(
                 in_=grouped_half[:].rearrange("p r t -> p (r t)"),
             )
 
-        x_flipped = flip_row(x_sb[:].bitcast(F32))
-        nc.scalar.copy(out=x_grouped[:].bitcast(F32), in_=x_flipped[:].rearrange("p u r -> p r u"))
-        quantise_half(1, x_grouped)
-
-        parts = [(t, relu, slice(P * a, P * (a + 1))) for t, relu, a in late_relus]
-        pieces = [(t, relu[:, cols]) for t, relu, cols in parts]
+        pieces = [(t, piece) for c, t, piece in late_relus if c < CHUNKS - 1]
         pieces += [(t, sums_v[:, t, a, :]) for a in (3, 2) for t in range(FEATURE_TILES)]
+        pieces += [(t, piece) for c, t, piece in late_relus if c == CHUNKS - 1]
         pieces += [(t, sums_g[:, i, a, :]) for i, t in enumerate(SHARED_TILES) for a in range(G_SLOTS)]
-        pieces += [(t, sums_v[:, t, a, :]) for a in (0, 1) for t in range(FEATURE_TILES)]
+        pieces += [(t, sums_v[:, t, a, :]) for t in range(FEATURE_TILES) for a in (0, 1)]
         agg_banks = []
         for t in range(FEATURE_TILES):
             agg_bank = flip_banks.tile([P, P], F32, tag="flipped")
@@ -291,6 +287,18 @@ def tile_graph_gan_pb_kernel(
                 start=t not in [other for other, _ in pieces[:i]],
                 stop=t not in [other for other, _ in pieces[i + 1 :]],
             )
+
+        x_flipped = flip_row(x_sb[:].bitcast(F32))
+        agg_sb = keep.tile([P, FEATURES], BF16)
+        for t in range(FEATURE_TILES):
+            cols = slice(P * t, P * (t + 1))
+            if t % 2 == 0:
+                nc.scalar.activation(out=agg_sb[:, cols], in_=agg_banks[t][:], func=ACT.Copy, scale=0.8)
+            else:
+                nc.vector.tensor_scalar_mul(out=agg_sb[:, cols], in0=agg_banks[t][:], scalar1=0.8)
+        agg_flipped = flip_row(agg_sb[:].bitcast(F32))
+        nc.scalar.copy(out=x_grouped[:].bitcast(F32), in_=x_flipped[:].rearrange("p u r -> p r u"))
+        quantise_half(1, x_grouped)
 
         node_sum = sum_banks.tile([P, FEATURES], F32, tag="sums")
 
@@ -306,15 +314,6 @@ def tile_graph_gan_pb_kernel(
             )
 
         node_matmul(1, True, False)
-
-        agg_sb = keep.tile([P, FEATURES], BF16)
-        for t in range(FEATURE_TILES):
-            cols = slice(P * t, P * (t + 1))
-            if t % 2 == 0:
-                nc.scalar.activation(out=agg_sb[:, cols], in_=agg_banks[t][:], func=ACT.Copy, scale=0.8)
-            else:
-                nc.vector.tensor_scalar_mul(out=agg_sb[:, cols], in0=agg_banks[t][:], scalar1=0.8)
-        agg_flipped = flip_row(agg_sb[:].bitcast(F32))
         agg_grouped = keep.tile([P, NODES, PACK], BF16, align_bytes=64)
         nc.scalar.copy(out=agg_grouped[:].bitcast(F32), in_=agg_flipped[:].rearrange("p u r -> p r u"))
         quantise_half(0, agg_grouped)

@@ -28,11 +28,13 @@ FEATURE_TILES = FEATURES // P
 CHUNK_TILES = [2] + [4] * 7 + [2]
 CHUNKS = len(CHUNK_TILES)
 SLOTS = 4
-G_SLOTS = 2
 assert sum(CHUNK_TILES) == NEIGHBOURS
 X_LOAD = CHUNKS - 4
-SHARED_TILES = [0, 1]
-LATE_TILES = {CHUNKS - 2: [2], CHUNKS - 1: [0, 1, 2, 3]}
+G_ROWS = {0: (0, 4), 1: (0, 4), 2: (0, 2)}
+G_ROWS_FIRST = {0: (0, 2), 1: (0, 2)}
+G_ROWS_LAST = {0: (0, 4), 1: (0, 4)}
+LATE_ROWS = {CHUNKS - 2: {2: (0, 4)}, CHUNKS - 1: {t: (0, 2) for t in range(FEATURE_TILES)}}
+G_WIDTH = P * sum(last - first for first, last in G_ROWS.values())
 HALF = FEATURES // 2
 SLOPE = 0.2
 
@@ -50,19 +52,23 @@ def tile_graph_gan_pb_kernel(
     def tiles_in_bank(c):
         return SLOTS // CHUNK_TILES[c]
 
-    def shared(c):
-        return SHARED_TILES if c < CHUNKS - 1 else []
+    def g_rows(c):
+        return {0: G_ROWS_FIRST, CHUNKS - 2: G_ROWS_LAST, CHUNKS - 1: {}}.get(c, G_ROWS)
 
-    def late(c):
-        return LATE_TILES.get(c, [])
+    def late_rows(c):
+        return LATE_ROWS.get(c, {})
+
+    def clamped_rows(c, t):
+        taken = max(rows.get(t, (0, 0))[1] for rows in (g_rows(c), late_rows(c)))
+        return (taken, CHUNK_TILES[c])
 
     with ExitStack() as ctx:
         ctx.enter_context(tc.manual_schedule())
         keep = ctx.enter_context(tc.tile_pool(name="keep", bufs=1))
         e2_pool = ctx.enter_context(tc.tile_pool(name="e2", bufs=CHUNKS))
         stage = ctx.enter_context(tc.tile_pool(name="stage", bufs=2))
-        relu_pool = ctx.enter_context(tc.tile_pool(name="relu", bufs=2 * len(SHARED_TILES)))
-        late_pool = ctx.enter_context(tc.tile_pool(name="late", bufs=sum(len(tiles) for tiles in LATE_TILES.values())))
+        relu_pool = ctx.enter_context(tc.tile_pool(name="relu", bufs=2))
+        late_pool = ctx.enter_context(tc.tile_pool(name="late", bufs=sum(len(rows) for rows in LATE_ROWS.values())))
         flip_banks = ctx.enter_context(tc.psum_pool(name="flip_banks", bufs=4))
         sum_banks = ctx.enter_context(tc.psum_pool(name="sum_banks", bufs=4))
 
@@ -71,7 +77,7 @@ def tile_graph_gan_pb_kernel(
         fn_words = keep.tile([P, PASSES, FEATURES], U32, align_bytes=64)
         fn_planes = keep.tile([P, PASSES, FEATURES], U8, align_bytes=64)
         sums_v = keep.tile([P, FEATURE_TILES, SLOTS, NODES], F32)
-        sums_g = keep.tile([P, len(SHARED_TILES), G_SLOTS, NODES], F32)
+        sums_g = keep.tile([P, G_WIDTH], F32)
         fe_bias_rows = keep.tile([P, P], BF16, align_bytes=64)
         nc.vector.memset(fe_bias_rows[:], 0.0)
         nc.scalar.dma_start(out=fe_bias_rows[0:FEATURE_TILES, :], in_=fe_b2.rearrange("(t p) -> t p", t=FEATURE_TILES))
@@ -119,6 +125,8 @@ def tile_graph_gan_pb_kernel(
 
         h_codes = keep.tile([P, PASSES, NODES], U32, align_bytes=64)
         h_scales = keep.tile([P, PASSES, NODES], U8, align_bytes=64)
+
+        late_relus = []
 
         def transpose_chunk(c):
             words = e2_tiles[c][:].bitcast(F32)
@@ -174,19 +182,28 @@ def tile_graph_gan_pb_kernel(
                     edge_sums.append(bank[:, i, :])
             return banks, edge_sums
 
-        def relu_on_scalar(c, edge_sums):
-            tiles = {}
-            for t in shared(c) + late(c):
-                if t in shared(c):
-                    relu = relu_pool.tile([P, P * CHUNK_TILES[c]], F32, tag="relu")
-                else:
-                    relu = late_pool.tile([P, P * CHUNK_TILES[c]], F32, tag="late")
-                nc.scalar.activation(out=relu[:], in_=edge_sums[t], func=ACT.Relu, bias=fe_bias[:, t : t + 1], scale=1.0)
-                tiles[t] = relu
-            return tiles
+        def g_columns(t, rows):
+            first = P * sum(G_ROWS[other][1] - G_ROWS[other][0] for other in G_ROWS if other < t)
+            return slice(first + P * rows[0], first + P * rows[1])
 
-        def slots_v(c, t):
-            return sums_v[:, t, 0 : CHUNK_TILES[c], :].rearrange("p a n -> p (a n)")
+        def relu_on_scalar(c, edge_sums):
+            def relu(out, t, rows):
+                nc.scalar.activation(
+                    out=out,
+                    in_=edge_sums[t][:, P * rows[0] : P * rows[1]],
+                    func=ACT.Relu,
+                    bias=fe_bias[:, t : t + 1],
+                    scale=1.0,
+                )
+
+            g_relu = relu_pool.tile([P, G_WIDTH], F32, tag="relu")
+            for t, rows in g_rows(c).items():
+                relu(g_relu[:, g_columns(t, rows)], t, rows)
+            for t, rows in late_rows(c).items():
+                late = late_pool.tile([P, SLOTS * NODES], F32, tag="late")
+                relu(late[:, 0 : P * (rows[1] - rows[0])], t, rows)
+                late_relus.extend([(c, t, late[:, P * i : P * (i + 1)]) for i in range(rows[1] - rows[0])])
+            return g_relu
 
         def add_linear(c, banks, k):
             first = k * tiles_in_bank(c)
@@ -194,24 +211,30 @@ def tile_graph_gan_pb_kernel(
             nc.vector.scalar_tensor_tensor(out=slots, in0=banks[k][:], scalar=0.25, in1=slots, op0=ALU.mult, op1=ALU.add)
 
         def add_clamped(c, edge_sums, t):
-            nc.vector.scalar_tensor_tensor(
-                out=slots_v(c, t),
-                in0=edge_sums[t],
-                scalar=fe_bias_negative[:, t : t + 1],
-                in1=slots_v(c, t),
-                op0=ALU.max,
-                op1=ALU.add,
-            )
+            first, last = clamped_rows(c, t)
+            if first < last:
+                slots = sums_v[:, t, first:last, :].rearrange("p a n -> p (a n)")
+                nc.vector.scalar_tensor_tensor(
+                    out=slots,
+                    in0=edge_sums[t][:, P * first : P * last],
+                    scalar=fe_bias_negative[:, t : t + 1],
+                    in1=slots,
+                    op0=ALU.max,
+                    op1=ALU.add,
+                )
 
-        def add_relu(c, relu_tiles):
-            width = G_SLOTS * NODES
-            for piece in range(CHUNK_TILES[c] // G_SLOTS):
-                for i, t in enumerate(SHARED_TILES):
-                    if t in relu_tiles:
-                        slots = sums_g[:, i, :, :].rearrange("p a n -> p (a n)")
-                        nc.gpsimd.tensor_tensor(
-                            out=slots, in0=slots, in1=relu_tiles[t][:, width * piece : width * (piece + 1)], op=ALU.add
-                        )
+        def add_relu(c, g_relu):
+            def add(columns):
+                sums, new = columns(sums_g), columns(g_relu)
+                nc.gpsimd.tensor_tensor(out=sums, in0=sums, in1=new, op=ALU.add)
+
+            whole = 2 * SLOTS * NODES
+            if c == 0:
+                add(lambda tile: tile[:, 0:whole].rearrange("p (t n) -> p t n", t=2)[:, :, 0 : P * CHUNK_TILES[c]])
+            elif g_rows(c) == G_ROWS_LAST:
+                add(lambda tile: tile[:, 0:whole])
+            elif g_rows(c):
+                add(lambda tile: tile[:])
 
         grouped = regroup_chunk(0, transpose_chunk(0))
 
@@ -225,7 +248,7 @@ def tile_graph_gan_pb_kernel(
         nc.vector.tensor_scalar_mul(out=fe_bias_negative[:], in0=fe_bias[:], scalar1=-1.0)
         fe_bias_start = keep.tile([P, FEATURE_TILES], F32)
         for t in range(FEATURE_TILES):
-            clamped = sum(CHUNK_TILES[c] for c in range(CHUNKS) if t not in shared(c) + late(c))
+            clamped = sum(clamped_rows(c, t)[1] - clamped_rows(c, t)[0] for c in range(CHUNKS))
             nc.vector.tensor_scalar_mul(
                 out=fe_bias_start[:, t : t + 1], in0=fe_bias[:, t : t + 1], scalar1=0.25 * NEIGHBOURS + clamped
             )
@@ -234,7 +257,6 @@ def tile_graph_gan_pb_kernel(
 
         x_grouped = keep.tile([P, NODES, PACK], BF16, align_bytes=64)
 
-        late_relus = []
         for c in range(CHUNKS):
             more = c + 1 < CHUNKS
             if more:
@@ -242,7 +264,7 @@ def tile_graph_gan_pb_kernel(
             banks, edge_sums = edge_matmuls(c, codes, scales)
             if more:
                 grouped = regroup_chunk(c + 1, flipped_banks)
-            relu_tiles = relu_on_scalar(c, edge_sums)
+            g_relu = relu_on_scalar(c, edge_sums)
             if more:
                 codes, scales = quantise_chunk(c + 1, grouped)
             previous = []
@@ -250,11 +272,10 @@ def tile_graph_gan_pb_kernel(
                 add_linear(c, banks, k)
                 for t in previous:
                     add_clamped(c, edge_sums, t)
-                previous = [t for t in range(k * tiles_in_bank(c), (k + 1) * tiles_in_bank(c)) if t not in relu_tiles]
+                previous = range(k * tiles_in_bank(c), (k + 1) * tiles_in_bank(c))
             for t in previous:
                 add_clamped(c, edge_sums, t)
-            add_relu(c, {t: relu_tiles[t] for t in shared(c)})
-            late_relus += [(c, t, relu_tiles[t][:, P * a : P * (a + 1)]) for t in late(c) for a in range(CHUNK_TILES[c])]
+            add_relu(c, g_relu)
 
         def flip_row(row_words):
             flipped = sum_banks.tile([P, PAIRS_OF_K, NODES], F32, tag="sums")
@@ -272,7 +293,9 @@ def tile_graph_gan_pb_kernel(
         pieces = [(t, piece) for c, t, piece in late_relus if c < CHUNKS - 1]
         pieces += [(t, sums_v[:, t, a, :]) for a in (3, 2) for t in range(FEATURE_TILES)]
         pieces += [(t, piece) for c, t, piece in late_relus if c == CHUNKS - 1]
-        pieces += [(t, sums_g[:, i, a, :]) for i, t in enumerate(SHARED_TILES) for a in range(G_SLOTS)]
+        for t in G_ROWS:
+            columns = sums_g[:, g_columns(t, G_ROWS[t])]
+            pieces += [(t, columns[:, P * i : P * (i + 1)]) for i in range(G_ROWS[t][1] - G_ROWS[t][0])]
         pieces += [(t, sums_v[:, t, a, :]) for t in range(FEATURE_TILES) for a in (0, 1)]
         agg_banks = []
         for t in range(FEATURE_TILES):

@@ -68,6 +68,7 @@ def tile_graph_gan_pb_kernel(
         e2_pool = ctx.enter_context(tc.tile_pool(name="e2", bufs=CHUNKS))
         stage = ctx.enter_context(tc.tile_pool(name="stage", bufs=2))
         relu_pool = ctx.enter_context(tc.tile_pool(name="relu", bufs=2))
+        sorted_pool = ctx.enter_context(tc.tile_pool(name="sorted", bufs=2))
         late_pool = ctx.enter_context(tc.tile_pool(name="late", bufs=sum(len(rows) for rows in LATE_ROWS.values())))
         flip_banks = ctx.enter_context(tc.psum_pool(name="flip_banks", bufs=4))
         sum_banks = ctx.enter_context(tc.psum_pool(name="sum_banks", bufs=4))
@@ -128,16 +129,24 @@ def tile_graph_gan_pb_kernel(
 
         late_relus = []
 
-        def transpose_chunk(c):
+        def sort_words(c):
+            words = e2_tiles[c][:].bitcast(F32)[:, CHUNK_TILES[c] - 1, :]
+            apart = sorted_pool.tile([P, PASSES, PAIRS_OF_K, P], F32, tag="sorted")
+            nc.scalar.copy(out=apart[:], in_=words.rearrange("p (g m u) -> p g u m", g=PASSES, u=PAIRS_OF_K))
+            return apart
+
+        def transpose_chunk(c, apart=None):
             words = e2_tiles[c][:].bitcast(F32)
             banks = []
             for a in range(CHUNK_TILES[c]):
                 flipped = flip_banks.tile([P, PASSES, PAIRS_OF_K, P], F32, tag="flipped")
                 for g in range(PASSES):
                     for u in range(PAIRS_OF_K):
+                        every_second = words[:, a, WORDS * g + u : WORDS * (g + 1) : PAIRS_OF_K]
+                        is_sorted = apart is not None and a == CHUNK_TILES[c] - 1
                         nc.tensor.transpose(
                             out=flipped[:, g, u, :],
-                            in_=words[:, a, WORDS * g + u : WORDS * (g + 1) : PAIRS_OF_K],
+                            in_=apart[:, g, u, :] if is_sorted else every_second,
                             identity=ident_f32[:],
                         )
                 banks.append(flipped)
@@ -257,14 +266,16 @@ def tile_graph_gan_pb_kernel(
 
         x_grouped = keep.tile([P, NODES, PACK], BF16, align_bytes=64)
 
+        apart = None
         for c in range(CHUNKS):
             more = c + 1 < CHUNKS
             if more:
-                flipped_banks = transpose_chunk(c + 1)
+                flipped_banks = transpose_chunk(c + 1, apart)
             banks, edge_sums = edge_matmuls(c, codes, scales)
             if more:
                 grouped = regroup_chunk(c + 1, flipped_banks)
             g_relu = relu_on_scalar(c, edge_sums)
+            apart = sort_words(c + 2) if c + 2 < CHUNKS - 1 else None
             if more:
                 codes, scales = quantise_chunk(c + 1, grouped)
             previous = []

@@ -33,7 +33,7 @@ X_LOAD = CHUNKS - 4
 G_ROWS = {0: (0, 4), 1: (0, 4), 2: (0, 2)}
 G_ROWS_FIRST = {0: (0, 2), 1: (0, 2)}
 G_ROWS_LAST = {0: (0, 4), 1: (0, 4)}
-LATE_ROWS = {CHUNKS - 2: {2: (0, 4)}, CHUNKS - 1: {t: (0, 2) for t in range(FEATURE_TILES)}}
+LATE_ROWS = {CHUNKS - 1: {t: (0, 2) for t in range(FEATURE_TILES)}}
 G_WIDTH = P * sum(last - first for first, last in G_ROWS.values())
 HALF = FEATURES // 2
 SLOPE = 0.2
@@ -81,28 +81,33 @@ def tile_graph_gan_pb_kernel(
         sums_g = keep.tile([P, G_WIDTH], F32)
         fe_bias_rows = keep.tile([P, P], BF16, align_bytes=64)
         nc.vector.memset(fe_bias_rows[:], 0.0)
-        nc.scalar.dma_start(out=fe_bias_rows[0:FEATURE_TILES, :], in_=fe_b2.rearrange("(t p) -> t p", t=FEATURE_TILES))
         warm = keep.tile([P, 2], F32)
         nc.vector.memset(warm[:], 0.0)
         nc.scalar.activation(out=warm[:, 1:2], in_=warm[:, 0:1], func=ACT.Relu)
         nc.vector.memset(fe_planes[:].bitcast(I32), 0)
         nc.vector.memset(fn_planes[:].bitcast(I32), 0)
-        nc.vector.memset(sums_v[:], 0.0)
+        nc.vector.memset(sums_v[:, :, CHUNK_TILES[0] :, :], 0.0)
 
         ident_f32 = keep.tile([P, P], F32)
         make_identity(nc, ident_f32[:])
         ident_bf16 = keep.tile([P, P], BF16, align_bytes=64)
         nc.gpsimd.tensor_copy(out=ident_bf16[:], in_=ident_f32[:])
         nc.gpsimd.memset(sums_g[:], 0.0)
+        bias_counts = keep.tile([P, FEATURE_TILES], F32)
+        for t in range(FEATURE_TILES):
+            clamped = sum(clamped_rows(c, t)[1] - clamped_rows(c, t)[0] for c in range(CHUNKS))
+            nc.gpsimd.memset(bias_counts[:, t : t + 1], (0.25 * NEIGHBOURS + clamped) / CHUNK_TILES[0])
 
         x_sb = keep.tile([P, FEATURES], BF16)
 
-        def load_weight(words_dram, scales_dram, words, planes):
+        def load_scales(scales_dram, planes):
             for quadrant in range(4):
                 nc.sync.dma_start(
                     out=planes[32 * quadrant : 32 * quadrant + 4, :, :].bitcast(I32),
                     in_=scales_dram.bitcast(I32)[:, 4 * quadrant : 4 * quadrant + 4, :].rearrange("g r n -> r g n"),
                 )
+
+        def load_words(words_dram, words):
             nc.sync.dma_start(
                 out=words[:].bitcast(I32),
                 in_=words_dram.rearrange("g p n t -> g p (n t)").bitcast(I32).rearrange("g p n -> p g n"),
@@ -114,13 +119,18 @@ def tile_graph_gan_pb_kernel(
             first_j = sum(CHUNK_TILES[:c])
             e2_sb = e2_pool.tile([P, tiles, EDGE_K], BF16, tag="e2")
             e2_tiles.append(e2_sb)
-            for a in range(tiles):
-                nc.sync.dma_start(out=e2_sb[:, a, :], in_=e2_nodes[:, first_j + a, :])
+            step = 2 if c == 1 else 1
+            for a in range(0, tiles, step):
+                nc.sync.dma_start(out=e2_sb[:, a : a + step, :], in_=e2_nodes[:, first_j + a : first_j + a + step, :])
             if c == 0:
-                load_weight(fe_w2_words, fe_w2_scales, fe_words, fe_planes)
+                load_scales(fe_w2_scales, fe_planes)
+            if c == 1:
+                load_words(fe_w2_words, fe_words)
+                nc.scalar.dma_start(out=fe_bias_rows[0:FEATURE_TILES, :], in_=fe_b2.rearrange("(t p) -> t p", t=FEATURE_TILES))
             if c == X_LOAD:
                 nc.sync.dma_start(out=x_sb[:], in_=x_rows)
-        load_weight(fn_w0_words, fn_w0_scales, fn_words, fn_planes)
+        load_scales(fn_w0_scales, fn_planes)
+        load_words(fn_w0_words, fn_words)
         fn_bias = keep.tile([P, FEATURES], BF16)
         nc.sync.dma_start(out=fn_bias[:], in_=fn_b0.partition_broadcast(P))
 
@@ -135,10 +145,10 @@ def tile_graph_gan_pb_kernel(
             nc.scalar.copy(out=apart[:], in_=words.rearrange("p (g m u) -> p g u m", g=PASSES, u=PAIRS_OF_K))
             return apart
 
-        def transpose_chunk(c, apart=None):
+        def transpose_tiles(c, tiles, apart=None):
             words = e2_tiles[c][:].bitcast(F32)
             banks = []
-            for a in range(CHUNK_TILES[c]):
+            for a in tiles:
                 flipped = flip_banks.tile([P, PASSES, PAIRS_OF_K, P], F32, tag="flipped")
                 for g in range(PASSES):
                     for u in range(PAIRS_OF_K):
@@ -152,14 +162,16 @@ def tile_graph_gan_pb_kernel(
                 banks.append(flipped)
             return banks
 
-        def regroup_chunk(c, banks):
+        def grouped_tile(c):
             grouped = stage.tile([P, PASSES, P * CHUNK_TILES[c], PACK], BF16, tag="grouped", align_bytes=64)
-            for a in range(CHUNK_TILES[c]):
+            return grouped
+
+        def regroup_tiles(grouped, tiles, banks):
+            for a, bank in zip(tiles, banks):
                 nc.scalar.copy(
                     out=grouped[:].bitcast(F32)[:, :, P * a : P * (a + 1), :],
-                    in_=banks[a][:].rearrange("p g u r -> p g r u"),
+                    in_=bank[:].rearrange("p g u r -> p g r u"),
                 )
-            return grouped
 
         def quantise_chunk(c, grouped):
             codes = stage.tile([P, PASSES, P * CHUNK_TILES[c]], U32, tag="codes", align_bytes=64)
@@ -211,8 +223,19 @@ def tile_graph_gan_pb_kernel(
             for t, rows in late_rows(c).items():
                 late = late_pool.tile([P, SLOTS * NODES], F32, tag="late")
                 relu(late[:, 0 : P * (rows[1] - rows[0])], t, rows)
-                late_relus.extend([(c, t, late[:, P * i : P * (i + 1)]) for i in range(rows[1] - rows[0])])
+                late_relus.extend([(t, late[:, P * i : P * (i + 1)]) for i in range(rows[1] - rows[0])])
             return g_relu
+
+        def start_sums(edge_sums):
+            for t in range(FEATURE_TILES):
+                nc.vector.tensor_scalar(
+                    out=sums_v[:, t, 0 : CHUNK_TILES[0], :].rearrange("p a n -> p (a n)"),
+                    in0=edge_sums[t],
+                    scalar1=0.25,
+                    scalar2=fe_bias_start[:, t : t + 1],
+                    op0=ALU.mult,
+                    op1=ALU.add,
+                )
 
         def add_linear(c, banks, k):
             first = k * tiles_in_bank(c)
@@ -245,39 +268,7 @@ def tile_graph_gan_pb_kernel(
             elif g_rows(c):
                 add(lambda tile: tile[:])
 
-        grouped = regroup_chunk(0, transpose_chunk(0))
-
-        codes, scales = quantise_chunk(0, grouped)
-
-        bias_flipped = flip_banks.tile([P, P], BF16, tag="flipped")
-        nc.tensor.transpose(out=bias_flipped[:], in_=fe_bias_rows[:], identity=ident_bf16[:])
-        fe_bias = keep.tile([P, FEATURE_TILES], F32)
-        nc.vector.tensor_copy(out=fe_bias[:], in_=bias_flipped[:, 0:FEATURE_TILES])
-        fe_bias_negative = keep.tile([P, FEATURE_TILES], F32)
-        nc.vector.tensor_scalar_mul(out=fe_bias_negative[:], in0=fe_bias[:], scalar1=-1.0)
-        fe_bias_start = keep.tile([P, FEATURE_TILES], F32)
-        for t in range(FEATURE_TILES):
-            clamped = sum(clamped_rows(c, t)[1] - clamped_rows(c, t)[0] for c in range(CHUNKS))
-            nc.vector.tensor_scalar_mul(
-                out=fe_bias_start[:, t : t + 1], in0=fe_bias[:, t : t + 1], scalar1=0.25 * NEIGHBOURS + clamped
-            )
-        for t in range(FEATURE_TILES):
-            nc.vector.tensor_scalar_add(out=sums_v[:, t, 0, :], in0=sums_v[:, t, 1, :], scalar1=fe_bias_start[:, t : t + 1])
-
-        x_grouped = keep.tile([P, NODES, PACK], BF16, align_bytes=64)
-
-        apart = None
-        for c in range(CHUNKS):
-            more = c + 1 < CHUNKS
-            if more:
-                flipped_banks = transpose_chunk(c + 1, apart)
-            banks, edge_sums = edge_matmuls(c, codes, scales)
-            if more:
-                grouped = regroup_chunk(c + 1, flipped_banks)
-            g_relu = relu_on_scalar(c, edge_sums)
-            apart = sort_words(c + 2) if c + 2 < CHUNKS - 1 else None
-            if more:
-                codes, scales = quantise_chunk(c + 1, grouped)
+        def add_chunk(c, banks, edge_sums, g_relu):
             previous = []
             for k in range(len(banks)):
                 add_linear(c, banks, k)
@@ -287,6 +278,45 @@ def tile_graph_gan_pb_kernel(
             for t in previous:
                 add_clamped(c, edge_sums, t)
             add_relu(c, g_relu)
+
+        first, second = range(CHUNK_TILES[0]), range(CHUNK_TILES[1])
+        grouped = grouped_tile(0)
+        regroup_tiles(grouped, first, transpose_tiles(0, first))
+        codes, scales = quantise_chunk(0, grouped)
+        grouped = grouped_tile(1)
+        regroup_tiles(grouped, second, transpose_tiles(1, second))
+        bias_flipped = flip_banks.tile([P, P], BF16, tag="flipped")
+        nc.tensor.transpose(out=bias_flipped[:], in_=fe_bias_rows[:], identity=ident_bf16[:])
+        banks, edge_sums = edge_matmuls(0, codes, scales)
+        fe_bias = keep.tile([P, FEATURE_TILES], F32)
+        nc.vector.tensor_copy(out=fe_bias[:], in_=bias_flipped[:, 0:FEATURE_TILES])
+        fe_bias_negative = keep.tile([P, FEATURE_TILES], F32)
+        nc.vector.tensor_scalar_mul(out=fe_bias_negative[:], in0=fe_bias[:], scalar1=-1.0)
+        fe_bias_start = keep.tile([P, FEATURE_TILES], F32)
+        nc.vector.tensor_tensor(out=fe_bias_start[:], in0=fe_bias[:], in1=bias_counts[:], op=ALU.mult)
+        g_relu = relu_on_scalar(0, edge_sums)
+        apart = None
+        codes, scales = quantise_chunk(1, grouped)
+        start_sums(edge_sums)
+        for t in range(FEATURE_TILES):
+            add_clamped(0, edge_sums, t)
+        add_relu(0, g_relu)
+
+        x_grouped = keep.tile([P, NODES, PACK], BF16, align_bytes=64)
+        for c in range(1, CHUNKS):
+            more = c + 1 < CHUNKS
+            if more:
+                next_tiles = range(CHUNK_TILES[c + 1])
+                flipped_banks = transpose_tiles(c + 1, next_tiles, apart)
+            banks, edge_sums = edge_matmuls(c, codes, scales)
+            if more:
+                grouped = grouped_tile(c + 1)
+                regroup_tiles(grouped, next_tiles, flipped_banks)
+            g_relu = relu_on_scalar(c, edge_sums)
+            apart = sort_words(c + 2) if c + 2 < CHUNKS - 1 else None
+            if more:
+                codes, scales = quantise_chunk(c + 1, grouped)
+            add_chunk(c, banks, edge_sums, g_relu)
 
         def flip_row(row_words):
             flipped = sum_banks.tile([P, PAIRS_OF_K, NODES], F32, tag="sums")
@@ -301,12 +331,12 @@ def tile_graph_gan_pb_kernel(
                 in_=grouped_half[:].rearrange("p r t -> p (r t)"),
             )
 
-        pieces = [(t, piece) for c, t, piece in late_relus if c < CHUNKS - 1]
-        pieces += [(t, sums_v[:, t, a, :]) for a in (3, 2) for t in range(FEATURE_TILES)]
-        pieces += [(t, piece) for c, t, piece in late_relus if c == CHUNKS - 1]
+        pieces = []
         for t in G_ROWS:
             columns = sums_g[:, g_columns(t, G_ROWS[t])]
             pieces += [(t, columns[:, P * i : P * (i + 1)]) for i in range(G_ROWS[t][1] - G_ROWS[t][0])]
+        pieces += [(t, piece) for t, piece in late_relus]
+        pieces += [(t, sums_v[:, t, a, :]) for a in (3, 2) for t in range(FEATURE_TILES)]
         pieces += [(t, sums_v[:, t, a, :]) for t in range(FEATURE_TILES) for a in (0, 1)]
         agg_banks = []
         for t in range(FEATURE_TILES):

@@ -33,7 +33,7 @@ X_LOAD = CHUNKS - 4
 G_ROWS = {0: (0, 4), 1: (0, 4), 2: (0, 2)}
 G_ROWS_FIRST = {0: (0, 2), 1: (0, 2)}
 G_ROWS_LAST = {0: (0, 4), 1: (0, 4)}
-LATE_ROWS = {CHUNKS - 1: {t: (0, 2) for t in range(FEATURE_TILES)}}
+LATE_ROWS = {CHUNKS - 2: {FEATURE_TILES - 1: (0, 2)}, CHUNKS - 1: {t: (0, 2) for t in range(FEATURE_TILES)}}
 G_WIDTH = P * sum(last - first for first, last in G_ROWS.values())
 HALF = FEATURES // 2
 SLOPE = 0.2
@@ -223,7 +223,7 @@ def tile_graph_gan_pb_kernel(
             for t, rows in late_rows(c).items():
                 late = late_pool.tile([P, SLOTS * NODES], F32, tag="late")
                 relu(late[:, 0 : P * (rows[1] - rows[0])], t, rows)
-                late_relus.extend([(t, late[:, P * i : P * (i + 1)]) for i in range(rows[1] - rows[0])])
+                late_relus.extend([(c, t, late[:, P * i : P * (i + 1)]) for i in range(rows[1] - rows[0])])
             return g_relu
 
         def start_sums(edge_sums):
@@ -331,11 +331,11 @@ def tile_graph_gan_pb_kernel(
                 in_=grouped_half[:].rearrange("p r t -> p (r t)"),
             )
 
-        pieces = []
+        pieces = [(t, piece) for c, t, piece in late_relus if c < CHUNKS - 1]
         for t in G_ROWS:
             columns = sums_g[:, g_columns(t, G_ROWS[t])]
             pieces += [(t, columns[:, P * i : P * (i + 1)]) for i in range(G_ROWS[t][1] - G_ROWS[t][0])]
-        pieces += [(t, piece) for t, piece in late_relus]
+        pieces += [(t, piece) for c, t, piece in late_relus if c == CHUNKS - 1]
         pieces += [(t, sums_v[:, t, a, :]) for a in (3, 2) for t in range(FEATURE_TILES)]
         pieces += [(t, sums_v[:, t, a, :]) for t in range(FEATURE_TILES) for a in (0, 1)]
         agg_banks = []
@@ -364,30 +364,34 @@ def tile_graph_gan_pb_kernel(
         nc.scalar.copy(out=x_grouped[:].bitcast(F32), in_=x_flipped[:].rearrange("p u r -> p r u"))
         quantise_half(1, x_grouped)
 
-        node_sum = sum_banks.tile([P, FEATURES], F32, tag="sums")
+        node_sums = []
+        for half in range(2):
+            node_sum = sum_banks.tile([P, HALF], F32, tag="sums")
+            node_sums.append(node_sum)
 
-        def node_matmul(g, first, last):
-            nc.tensor.matmul_mx(
-                out=node_sum[:],
-                lhsT=h_codes[:, g, :].bitcast(FP8X4),
-                lhsT_scale=h_scales[:, g, :],
-                rhs=fn_words[:, g, :].bitcast(FP8X4),
-                rhs_scale=fn_planes[:, g, :],
-                start=first,
-                stop=last,
-            )
+        def node_matmuls(g, first, last):
+            for half in range(2):
+                nc.tensor.matmul_mx(
+                    out=node_sums[half][:],
+                    lhsT=h_codes[:, g, :].bitcast(FP8X4),
+                    lhsT_scale=h_scales[:, g, :],
+                    rhs=fn_words[:, g, HALF * half : HALF * (half + 1)].bitcast(FP8X4),
+                    rhs_scale=fn_planes[:, g, HALF * half : HALF * (half + 1)],
+                    start=first,
+                    stop=last,
+                )
 
-        node_matmul(1, True, False)
+        node_matmuls(1, True, False)
         agg_grouped = keep.tile([P, NODES, PACK], BF16, align_bytes=64)
         nc.scalar.copy(out=agg_grouped[:].bitcast(F32), in_=agg_flipped[:].rearrange("p u r -> p r u"))
         quantise_half(0, agg_grouped)
-        node_matmul(0, False, True)
+        node_matmuls(0, False, True)
 
         biased = keep.tile([P, FEATURES], F32)
         result = keep.tile([P, FEATURES], F32)
         for half in range(2):
             cols = slice(HALF * half, HALF * (half + 1))
-            nc.vector.tensor_tensor(out=biased[:, cols], in0=node_sum[:, cols], in1=fn_bias[:, cols], op=ALU.add)
+            nc.vector.tensor_tensor(out=biased[:, cols], in0=node_sums[half][:], in1=fn_bias[:, cols], op=ALU.add)
         for half in range(2):
             cols = slice(HALF * half, HALF * (half + 1))
             nc.vector.scalar_tensor_tensor(

from contextlib import ExitStack

import concourse.mybir as mybir
from concourse.masks import make_identity

F32 = mybir.dt.float32
BF16 = mybir.dt.bfloat16
I32 = mybir.dt.int32
U32 = mybir.dt.uint32
U8 = mybir.dt.uint8
FP8X4 = mybir.dt.float8_e4m3fn_x4
ALU = mybir.AluOpType
ACT = mybir.ActivationFunctionType

P = 128
PACK = 4
K_PASS = P * PACK
PASSES = 2
PAIRS_OF_K = 2
WORDS = K_PASS // 2

NEIGHBOURS = 32
NODES = 128
EDGE_K = 1024
FEATURES = 512
FEATURE_TILES = FEATURES // P

CHUNK_TILES = [2] + [4] * 7 + [2]
CHUNKS = len(CHUNK_TILES)
SLOTS = 4
assert sum(CHUNK_TILES) == NEIGHBOURS
X_LOAD = CHUNKS - 4
G_ROWS = {0: (0, 4), 1: (0, 4), 2: (0, 2)}
G_ROWS_FIRST = {0: (0, 2), 1: (0, 2)}
G_ROWS_LAST = {0: (0, 4), 1: (0, 4)}
LATE_ROWS = {CHUNKS - 2: {FEATURE_TILES - 1: (0, 2)}, CHUNKS - 1: {t: (0, 2) for t in range(FEATURE_TILES)}}
G_WIDTH = P * sum(last - first for first, last in G_ROWS.values())
HALF = FEATURES // 2
SLOPE = 0.2

FLOPS = 2 * NODES * NEIGHBOURS * EDGE_K * FEATURES + 2 * NODES * (2 * FEATURES) * FEATURES


def tile_graph_gan_pb_kernel(
    tc, e2, x, fe_w2_words, fe_w2_scales, fe_b2, fn_w0_words, fn_w0_scales, fn_b0, out
):
    nc = tc.nc
    e2_nodes = e2.rearrange("b i j k -> (b i) j k")
    x_rows = x.rearrange("b i d -> (b i) d")
    out_rows = out.rearrange("b i f -> (b i) f")

    def tiles_in_bank(c):
        return SLOTS // CHUNK_TILES[c]

    def g_rows(c):
        return {0: G_ROWS_FIRST, CHUNKS - 2: G_ROWS_LAST, CHUNKS - 1: {}}.get(c, G_ROWS)

    def late_rows(c):
        return LATE_ROWS.get(c, {})

    def clamped_rows(c, t):
        taken = max(rows.get(t, (0, 0))[1] for rows in (g_rows(c), late_rows(c)))
        return (taken, CHUNK_TILES[c])

    with ExitStack() as ctx:
        ctx.enter_context(tc.manual_schedule())
        keep = ctx.enter_context(tc.tile_pool(name="keep", bufs=1))
        e2_pool = ctx.enter_context(tc.tile_pool(name="e2", bufs=CHUNKS))
        stage = ctx.enter_context(tc.tile_pool(name="stage", bufs=2))
        relu_pool = ctx.enter_context(tc.tile_pool(name="relu", bufs=2))
        sorted_pool = ctx.enter_context(tc.tile_pool(name="sorted", bufs=2))
        late_pool = ctx.enter_context(tc.tile_pool(name="late", bufs=sum(len(rows) for rows in LATE_ROWS.values())))
        flip_banks = ctx.enter_context(tc.psum_pool(name="flip_banks", bufs=4))
        sum_banks = ctx.enter_context(tc.psum_pool(name="sum_banks", bufs=4))

        fe_words = keep.tile([P, PASSES, FEATURES], U32, align_bytes=64)
        fe_planes = keep.tile([P, PASSES, FEATURES], U8, align_bytes=64)
        fn_words = keep.tile([P, PASSES, FEATURES], U32, align_bytes=64)
        fn_planes = keep.tile([P, PASSES, FEATURES], U8, align_bytes=64)
        sums_v = keep.tile([P, FEATURE_TILES, SLOTS, NODES], F32)
        sums_g = keep.tile([P, G_WIDTH], F32)
        fe_bias_rows = keep.tile([P, P], BF16, align_bytes=64)
        nc.vector.memset(fe_bias_rows[:], 0.0)
        warm = keep.tile([P, 2], F32)
        nc.vector.memset(warm[:], 0.0)
        nc.scalar.activation(out=warm[:, 1:2], in_=warm[:, 0:1], func=ACT.Relu)
        nc.vector.memset(fe_planes[:].bitcast(I32), 0)
        nc.vector.memset(fn_planes[:].bitcast(I32), 0)
        nc.vector.memset(sums_v[:, :, CHUNK_TILES[0] :, :], 0.0)

        ident_f32 = keep.tile([P, P], F32)
        make_identity(nc, ident_f32[:])
        ident_bf16 = keep.tile([P, P], BF16, align_bytes=64)
        nc.gpsimd.tensor_copy(out=ident_bf16[:], in_=ident_f32[:])
        nc.gpsimd.memset(sums_g[:], 0.0)
        bias_counts = keep.tile([P, FEATURE_TILES], F32)
        for t in range(FEATURE_TILES):
            clamped = sum(clamped_rows(c, t)[1] - clamped_rows(c, t)[0] for c in range(CHUNKS))
            nc.gpsimd.memset(bias_counts[:, t : t + 1], (0.25 * NEIGHBOURS + clamped) / CHUNK_TILES[0])

        x_sb = keep.tile([P, FEATURES], BF16)

        def load_scales(scales_dram, planes):
            for quadrant in range(4):
                nc.sync.dma_start(
                    out=planes[32 * quadrant : 32 * quadrant + 4, :, :].bitcast(I32),
                    in_=scales_dram.bitcast(I32)[:, 4 * quadrant : 4 * quadrant + 4, :].rearrange("g r n -> r g n"),
                )

        def load_words(words_dram, words):
            nc.sync.dma_start(
                out=words[:].bitcast(I32),
                in_=words_dram.rearrange("g p n t -> g p (n t)").bitcast(I32).rearrange("g p n -> p g n"),
            )

        e2_tiles = []
        for c in range(CHUNKS):
            tiles = CHUNK_TILES[c]
            first_j = sum(CHUNK_TILES[:c])
            e2_sb = e2_pool.tile([P, tiles, EDGE_K], BF16, tag="e2")
            e2_tiles.append(e2_sb)
            step = 2 if c == 1 else 1
            for a in range(0, tiles, step):
                nc.sync.dma_start(out=e2_sb[:, a : a + step, :], in_=e2_nodes[:, first_j + a : first_j + a + step, :])
            if c == 0:
                load_scales(fe_w2_scales, fe_planes)
            if c == 1:
                load_words(fe_w2_words, fe_words)
                nc.scalar.dma_start(out=fe_bias_rows[0:FEATURE_TILES, :], in_=fe_b2.rearrange("(t p) -> t p", t=FEATURE_TILES))
            if c == X_LOAD:
                nc.sync.dma_start(out=x_sb[:], in_=x_rows)
        load_scales(fn_w0_scales, fn_planes)
        load_words(fn_w0_words, fn_words)
        fn_bias = keep.tile([P, FEATURES], BF16)
        nc.sync.dma_start(out=fn_bias[:], in_=fn_b0.partition_broadcast(P))

        h_codes = keep.tile([P, PASSES, NODES], U32, align_bytes=64)
        h_scales = keep.tile([P, PASSES, NODES], U8, align_bytes=64)

        late_relus = []

        def sort_words(c):
            words = e2_tiles[c][:].bitcast(F32)[:, CHUNK_TILES[c] - 1, :]
            apart = sorted_pool.tile([P, PASSES, PAIRS_OF_K, P], F32, tag="sorted")
            nc.scalar.copy(out=apart[:], in_=words.rearrange("p (g m u) -> p g u m", g=PASSES, u=PAIRS_OF_K))
            return apart

        def transpose_tiles(c, tiles, apart=None):
            words = e2_tiles[c][:].bitcast(F32)
            banks = []
            for a in tiles:
                flipped = flip_banks.tile([P, PASSES, PAIRS_OF_K, P], F32, tag="flipped")
                for g in range(PASSES):
                    for u in range(PAIRS_OF_K):
                        every_second = words[:, a, WORDS * g + u : WORDS * (g + 1) : PAIRS_OF_K]
                        is_sorted = apart is not None and a == CHUNK_TILES[c] - 1
                        nc.tensor.transpose(
                            out=flipped[:, g, u, :],
                            in_=apart[:, g, u, :] if is_sorted else every_second,
                            identity=ident_f32[:],
                        )
                banks.append(flipped)
            return banks

        def grouped_tile(c):
            grouped = stage.tile([P, PASSES, P * CHUNK_TILES[c], PACK], BF16, tag="grouped", align_bytes=64)
            return grouped

        def regroup_tiles(grouped, tiles, banks):
            for a, bank in zip(tiles, banks):
                nc.scalar.copy(
                    out=grouped[:].bitcast(F32)[:, :, P * a : P * (a + 1), :],
                    in_=bank[:].rearrange("p g u r -> p g r u"),
                )

        def quantise_chunk(c, grouped):
            codes = stage.tile([P, PASSES, P * CHUNK_TILES[c]], U32, tag="codes", align_bytes=64)
            scales = stage.tile([P, PASSES, P * CHUNK_TILES[c]], U8, tag="scales", align_bytes=64)
            nc.vector.quantize_mx(
                out=codes[:].rearrange("p g c -> p (g c)").bitcast(FP8X4),
                scales=scales[:].rearrange("p g c -> p (g c)"),
                in_=grouped[:].rearrange("p g c t -> p (g c t)"),
            )
            return codes, scales

        def edge_matmuls(c, codes, scales):
            banks, edge_sums = [], []
            for first in range(0, FEATURE_TILES, tiles_in_bank(c)):
                bank = sum_banks.tile([P, tiles_in_bank(c), P * CHUNK_TILES[c]], F32, tag="sums")
                banks.append(bank)
                for i in range(tiles_in_bank(c)):
                    t = first + i
                    for g in range(PASSES):
                        nc.tensor.matmul_mx(
                            out=bank[:, i, :],
                            lhsT=fe_words[:, g, P * t : P * (t + 1)].bitcast(FP8X4),
                            lhsT_scale=fe_planes[:, g, P * t : P * (t + 1)],
                            rhs=codes[:, g, :].bitcast(FP8X4),
                            rhs_scale=scales[:, g, :],
                            start=(g == 0),
                            stop=(g == PASSES - 1),
                        )
                    edge_sums.append(bank[:, i, :])
            return banks, edge_sums

        def g_columns(t, rows):
            first = P * sum(G_ROWS[other][1] - G_ROWS[other][0] for other in G_ROWS if other < t)
            return slice(first + P * rows[0], first + P * rows[1])

        def relu_on_scalar(c, edge_sums):
            def relu(out, t, rows):
                nc.scalar.activation(
                    out=out,
                    in_=edge_sums[t][:, P * rows[0] : P * rows[1]],
                    func=ACT.Relu,
                    bias=fe_bias[:, t : t + 1],
                    scale=1.0,
                )

            g_relu = relu_pool.tile([P, G_WIDTH], F32, tag="relu")
            for t, rows in g_rows(c).items():
                relu(g_relu[:, g_columns(t, rows)], t, rows)
            for t, rows in late_rows(c).items():
                late = late_pool.tile([P, SLOTS * NODES], F32, tag="late")
                relu(late[:, 0 : P * (rows[1] - rows[0])], t, rows)
                late_relus.extend([(c, t, late[:, P * i : P * (i + 1)]) for i in range(rows[1] - rows[0])])
            return g_relu

        def start_sums(edge_sums):
            for t in range(FEATURE_TILES):
                nc.vector.tensor_scalar(
                    out=sums_v[:, t, 0 : CHUNK_TILES[0], :].rearrange("p a n -> p (a n)"),
                    in0=edge_sums[t],
                    scalar1=0.25,
                    scalar2=fe_bias_start[:, t : t + 1],
                    op0=ALU.mult,
                    op1=ALU.add,
                )

        def add_linear(c, banks, k):
            first = k * tiles_in_bank(c)
            slots = sums_v[:, first : first + tiles_in_bank(c), 0 : CHUNK_TILES[c], :].rearrange("p t a n -> p t (a n)")
            nc.vector.scalar_tensor_tensor(out=slots, in0=banks[k][:], scalar=0.25, in1=slots, op0=ALU.mult, op1=ALU.add)

        def add_clamped(c, edge_sums, t):
            first, last = clamped_rows(c, t)
            if first < last:
                slots = sums_v[:, t, first:last, :].rearrange("p a n -> p (a n)")
                nc.vector.scalar_tensor_tensor(
                    out=slots,
                    in0=edge_sums[t][:, P * first : P * last],
                    scalar=fe_bias_negative[:, t : t + 1],
                    in1=slots,
                    op0=ALU.max,
                    op1=ALU.add,
                )

        def add_relu(c, g_relu):
            def add(columns):
                sums, new = columns(sums_g), columns(g_relu)
                nc.gpsimd.tensor_tensor(out=sums, in0=sums, in1=new, op=ALU.add)

            whole = 2 * SLOTS * NODES
            if c == 0:
                add(lambda tile: tile[:, 0:whole].rearrange("p (t n) -> p t n", t=2)[:, :, 0 : P * CHUNK_TILES[c]])
            elif g_rows(c) == G_ROWS_LAST:
                add(lambda tile: tile[:, 0:whole])
            elif g_rows(c):
                add(lambda tile: tile[:])

        def add_chunk(c, banks, edge_sums, g_relu):
            previous = []
            for k in range(len(banks)):
                add_linear(c, banks, k)
                for t in previous:
                    add_clamped(c, edge_sums, t)
                previous = range(k * tiles_in_bank(c), (k + 1) * tiles_in_bank(c))
            for t in previous:
                add_clamped(c, edge_sums, t)
            add_relu(c, g_relu)

        first, second = range(CHUNK_TILES[0]), range(CHUNK_TILES[1])
        grouped = grouped_tile(0)
        regroup_tiles(grouped, first, transpose_tiles(0, first))
        codes, scales = quantise_chunk(0, grouped)
        grouped = grouped_tile(1)
        regroup_tiles(grouped, second, transpose_tiles(1, second))
        bias_flipped = flip_banks.tile([P, P], BF16, tag="flipped")
        nc.tensor.transpose(out=bias_flipped[:], in_=fe_bias_rows[:], identity=ident_bf16[:])
        banks, edge_sums = edge_matmuls(0, codes, scales)
        fe_bias = keep.tile([P, FEATURE_TILES], F32)
        nc.vector.tensor_copy(out=fe_bias[:], in_=bias_flipped[:, 0:FEATURE_TILES])
        fe_bias_negative = keep.tile([P, FEATURE_TILES], F32)
        nc.vector.tensor_scalar_mul(out=fe_bias_negative[:], in0=fe_bias[:], scalar1=-1.0)
        fe_bias_start = keep.tile([P, FEATURE_TILES], F32)
        nc.vector.tensor_tensor(out=fe_bias_start[:], in0=fe_bias[:], in1=bias_counts[:], op=ALU.mult)
        g_relu = relu_on_scalar(0, edge_sums)
        apart = None
        codes, scales = quantise_chunk(1, grouped)
        start_sums(edge_sums)
        for t in range(FEATURE_TILES):
            add_clamped(0, edge_sums, t)
        add_relu(0, g_relu)

        x_grouped = keep.tile([P, NODES, PACK], BF16, align_bytes=64)
        for c in range(1, CHUNKS):
            more = c + 1 < CHUNKS
            if more:
                next_tiles = range(CHUNK_TILES[c + 1])
                flipped_banks = transpose_tiles(c + 1, next_tiles, apart)
            banks, edge_sums = edge_matmuls(c, codes, scales)
            if more:
                grouped = grouped_tile(c + 1)
                regroup_tiles(grouped, next_tiles, flipped_banks)
            g_relu = relu_on_scalar(c, edge_sums)
            apart = sort_words(c + 2) if c + 2 < CHUNKS - 1 else None
            if more:
                codes, scales = quantise_chunk(c + 1, grouped)
            add_chunk(c, banks, edge_sums, g_relu)

        def flip_row(row_words):
            flipped = sum_banks.tile([P, PAIRS_OF_K, NODES], F32, tag="sums")
            for u in range(PAIRS_OF_K):
                nc.tensor.transpose(out=flipped[:, u, :], in_=row_words[:, u:WORDS:PAIRS_OF_K], identity=ident_f32[:])
            return flipped

        def quantise_half(g, grouped_half):
            nc.vector.quantize_mx(
                out=h_codes[:, g, :].bitcast(FP8X4),
                scales=h_scales[:, g, :],
                in_=grouped_half[:].rearrange("p r t -> p (r t)"),
            )

        pieces = [(t, piece) for c, t, piece in late_relus if c < CHUNKS - 1]
        for t in G_ROWS:
            columns = sums_g[:, g_columns(t, G_ROWS[t])]
            pieces += [(t, columns[:, P * i : P * (i + 1)]) for i in range(G_ROWS[t][1] - G_ROWS[t][0])]
        pieces += [(t, piece) for c, t, piece in late_relus if c == CHUNKS - 1]
        pieces += [(t, sums_v[:, t, a, :]) for a in (3, 2) for t in range(FEATURE_TILES)]
        pieces += [(t, sums_v[:, t, a, :]) for t in range(FEATURE_TILES) for a in (0, 1)]
        agg_banks = []
        for t in range(FEATURE_TILES):
            agg_bank = flip_banks.tile([P, P], F32, tag="flipped")
            agg_banks.append(agg_bank)
        for i, (t, piece) in enumerate(pieces):
            nc.tensor.matmul(
                out=agg_banks[t][:],
                lhsT=piece,
                rhs=ident_f32[:],
                is_transpose=True,
                start=t not in [other for other, _ in pieces[:i]],
                stop=t not in [other for other, _ in pieces[i + 1 :]],
            )

        x_flipped = flip_row(x_sb[:].bitcast(F32))
        agg_sb = keep.tile([P, FEATURES], BF16)
        for t in range(FEATURE_TILES):
            cols = slice(P * t, P * (t + 1))
            if t % 2 == 0:
                nc.scalar.activation(out=agg_sb[:, cols], in_=agg_banks[t][:], func=ACT.Copy, scale=0.8)
            else:
                nc.vector.tensor_scalar_mul(out=agg_sb[:, cols], in0=agg_banks[t][:], scalar1=0.8)
        agg_flipped = flip_row(agg_sb[:].bitcast(F32))
        nc.scalar.copy(out=x_grouped[:].bitcast(F32), in_=x_flipped[:].rearrange("p u r -> p r u"))
        quantise_half(1, x_grouped)

        node_sums = []
        for half in range(2):
            node_sum = sum_banks.tile([P, HALF], F32, tag="sums")
            node_sums.append(node_sum)

        def node_matmuls(g, first, last):
            for half in range(2):
                nc.tensor.matmul_mx(
                    out=node_sums[half][:],
                    lhsT=h_codes[:, g, :].bitcast(FP8X4),
                    lhsT_scale=h_scales[:, g, :],
                    rhs=fn_words[:, g, HALF * half : HALF * (half + 1)].bitcast(FP8X4),
                    rhs_scale=fn_planes[:, g, HALF * half : HALF * (half + 1)],
                    start=first,
                    stop=last,
                )

        node_matmuls(1, True, False)
        agg_grouped = keep.tile([P, NODES, PACK], BF16, align_bytes=64)
        nc.scalar.copy(out=agg_grouped[:].bitcast(F32), in_=agg_flipped[:].rearrange("p u r -> p r u"))
        quantise_half(0, agg_grouped)
        node_matmuls(0, False, True)

        biased = keep.tile([P, FEATURES], F32)
        result = keep.tile([P, FEATURES], F32)
        for half in range(2):
            cols = slice(HALF * half, HALF * (half + 1))
            nc.vector.tensor_tensor(out=biased[:, cols], in0=node_sums[half][:], in1=fn_bias[:, cols], op=ALU.add)
        for half in range(2):
            cols = slice(HALF * half, HALF * (half + 1))
            nc.vector.scalar_tensor_tensor(
                out=result[:, cols],
                in0=biased[:, cols],
                scalar=SLOPE,
                in1=biased[:, cols],
                op0=ALU.mult,
                op1=ALU.max,
            )
            nc.sync.dma_start(out=out_rows[:, cols], in_=result[:, cols])
